import numpy as np
import ml_dtypes


def mxq(x, axis, fmt="e4m3"):
    dtype, down = {"e4m3": (ml_dtypes.float8_e4m3fn, 7), "e5m2": (ml_dtypes.float8_e5m2, 14)}[fmt]
    v = np.moveaxis(np.asarray(x, np.float32).astype(ml_dtypes.bfloat16).astype(np.float64), axis, -1)
    blocks = v.reshape(v.shape[:-1] + (-1, 32))
    amax = np.abs(blocks).max(-1, keepdims=True)
    byte = np.maximum(np.where(amax > 0, np.frexp(amax)[1] - 1 + 127, 0) - down, 1)
    scale = np.exp2(byte - 127.0)
    codes = (blocks / scale).astype(np.float32).astype(dtype).astype(np.float64)
    return np.moveaxis((codes * scale).reshape(v.shape), -1, axis)


WIDE = False


def mx_kscale(k):
    if not WIDE:
        return np.ones(k)
    levels = np.array([10, -10, 5, -5, 0])
    a = np.random.permutation(np.resize(levels, k // 512 * 4)).reshape(k // 512, 4)
    idx = np.arange(k)
    return np.exp2(a[idx // 512, idx % 128 // 32])


BF16 = ml_dtypes.bfloat16


def bf(x):
    return np.asarray(x, np.float32).astype(BF16)


def f64(x):
    return np.asarray(x).astype(np.float64)


E2M1 = np.array([0.0, 0.5, 1.0, 1.5, 2.0, 3.0, 4.0, 6.0, -0.0, -0.5, -1.0, -1.5, -2.0, -3.0, -4.0, -6.0])


def pack_weight(w, fmt):
    k, n = w.shape
    w = f64(bf(w)).reshape(k // 32, 32, n)
    amax = np.abs(w).max(1)
    if fmt == "e4m3":
        byte = np.frexp(amax)[1] - 1 + 127 - 7
    else:
        mant, ex = np.frexp(amax / 6.0)
        byte = np.where(mant > 0.5, ex, ex - 1) + 127
    byte = np.clip(np.where(amax > 0, byte, 1), 1, 254)
    scaled = (w * np.exp2(127.0 - byte)[:, None, :]).reshape(k, n).astype(np.float32)
    by_word = np.ascontiguousarray(scaled.reshape(k // 512, 128, 4, n).transpose(0, 1, 3, 2))
    if fmt == "e4m3":
        words = by_word.astype(ml_dtypes.float8_e4m3fn).view(np.uint8)
    else:
        c = by_word.astype(ml_dtypes.float4_e2m1fn).view(np.uint8) & 0xF
        words = c[..., 0::2] | (c[..., 1::2] << 4)
    return np.ascontiguousarray(words), np.ascontiguousarray(byte.astype(np.uint8).reshape(k // 512, 16, n))


def unpack_weight(words, scales, fmt):
    g, p, n, _ = words.shape
    if fmt == "e4m3":
        vals = np.ascontiguousarray(words).view(ml_dtypes.float8_e4m3fn).astype(np.float64)
    else:
        nib = np.empty((g, p, n, 4), np.uint8)
        nib[..., 0::2] = words & 0xF
        nib[..., 1::2] = words >> 4
        vals = E2M1[nib]
    vals = vals * np.repeat(np.exp2(scales.astype(np.float64) - 127.0), 8, axis=1)[..., None]
    return vals.transpose(0, 1, 3, 2).reshape(g * 512, n)


B, C, L = 64, 16, 4096
LEVEL = 3
NODES = 2 ** LEVEL
D = L // NODES
INV_SQRT2 = 0.7071067811865476


def haar_wpt(x, level):
    c = x[:, :, None, :]
    for _ in range(level):
        Bn, Cn, N, n = c.shape
        y = c.reshape(Bn, Cn, N, n // 2, 2)
        a = (y[..., 0] + y[..., 1]) * INV_SQRT2
        d = (y[..., 0] - y[..., 1]) * INV_SQRT2
        c = np.stack([a, d], axis=3).reshape(Bn, Cn, N * 2, n // 2)
    return c


def haar_iwpt(c, level):
    for _ in range(level):
        a = c[:, :, 0::2, :]
        d = c[:, :, 1::2, :]
        even = (a + d) * INV_SQRT2
        odd = (a - d) * INV_SQRT2
        Bn, Cn, N2, n = even.shape
        c = np.stack([even, odd], axis=-1).reshape(Bn, Cn, N2, 2 * n)
    return c[:, :, 0, :]


def setup_inputs():
    s = mx_kscale(D)
    x = bf(np.random.standard_normal((B, C, L)) * np.repeat(s, NODES))
    w = np.random.standard_normal((D, D)) / np.sqrt(D) / s[None, :]
    words, scales = pack_weight(np.ascontiguousarray(w.T), "e4m3")
    b = bf(np.random.standard_normal(D) * 0.1)
    threshold = bf(np.random.uniform(0.08, 0.12, 1))
    return {"x": x,
            "W_words": words,
            "W_scales": scales,
            "b": b,
            "threshold": threshold}


def reference(x, W_words, W_scales, b, threshold):
    x = f64(x)
    coeffs = haar_wpt(x, LEVEL)
    z = (mxq(coeffs, 3, "e4m3") @ unpack_weight(W_words, W_scales, "e4m3")) + f64(b)
    gate = 1.0 / (1.0 + np.exp(-z))
    gated = coeffs * gate
    gated = np.where(np.abs(gated) < f64(threshold), 0.0, gated)
    recon = haar_iwpt(gated, LEVEL)
    return recon + x

@@ -1,0 +1,239 @@
+from contextlib import ExitStack
+
+import concourse.mybir as mybir
+from concourse.masks import make_identity
+
+F32 = mybir.dt.float32
+BF16 = mybir.dt.bfloat16
+I32 = mybir.dt.int32
+U32 = mybir.dt.uint32
+U8 = mybir.dt.uint8
+FP8X4 = mybir.dt.float8_e4m3fn_x4
+ALU = mybir.AluOpType
+ACT = mybir.ActivationFunctionType
+
+P = 128
+L = 4096
+NODES = 8
+D = L // NODES
+PACK = 4
+E_BLOCKS = D // P
+N_MOVING = 512
+ROWS = 64 * 16
+ROW_TILES = ROWS // P
+
+FLOPS = 2 * ROWS * NODES * D * D
+
+
+def butterfly(nc, out_sum, out_diff, first, second):
+    nc.vector.tensor_tensor(out=out_sum, in0=first, in1=second, op=ALU.add)
+    nc.vector.tensor_tensor(out=out_diff, in0=first, in1=second, op=ALU.subtract)
+
+
+def tile_waveletgatednet_kernel(tc, x, W_words, W_scales, b, threshold, out):
+    nc = tc.nc
+    x_rows = x.flatten_outer_dims()
+    out_rows = out.flatten_outer_dims()
+
+    with ExitStack() as ctx:
+        const = ctx.enter_context(tc.tile_pool(name="const", bufs=1))
+        sbuf = ctx.enter_context(tc.tile_pool(name="sbuf", bufs=1))
+        psum = ctx.enter_context(tc.psum_pool(name="psum", bufs=2))
+
+        ident_f32 = const.tile([P, P], F32)
+        make_identity(nc, ident_f32[:])
+        ident_bf16 = const.tile([P, P], BF16)
+        make_identity(nc, ident_bf16[:])
+
+        w_codes = const.tile([P, D], U32, align_bytes=64)
+        nc.sync.dma_start(
+            out=w_codes[:].bitcast(I32),
+            in_=W_words[0].rearrange("p e t -> p (e t)").bitcast(I32),
+        )
+        w_scales = const.tile([P, D], U8, align_bytes=64)
+        nc.vector.memset(w_scales[:].bitcast(I32), 0)
+        for quadrant in range(4):
+            nc.sync.dma_start(
+                out=w_scales[32 * quadrant : 32 * quadrant + 4, :].bitcast(I32),
+                in_=W_scales[0, 4 * quadrant : 4 * quadrant + 4, :].bitcast(I32),
+            )
+
+        b_rows = const.tile([P, P], BF16)
+        nc.vector.memset(b_rows[:], 0.0)
+        nc.sync.dma_start(out=b_rows[0:E_BLOCKS, :], in_=b.rearrange("(k e) -> k e", e=P))
+        b_cols = psum.tile([P, P], BF16, tag="flipped")
+        nc.tensor.transpose(b_cols[:], b_rows[:], ident_bf16[:])
+        bias = const.tile([P, E_BLOCKS], F32)
+        nc.vector.tensor_copy(out=bias[:], in_=b_cols[:, 0:E_BLOCKS])
+
+        thr_bf16 = const.tile([P, 1], BF16)
+        nc.sync.dma_start(out=thr_bf16[:], in_=threshold.partition_broadcast(P))
+        thr = const.tile([P, 1], F32)
+        nc.vector.tensor_copy(out=thr[:], in_=thr_bf16[:])
+        thr_sq = const.tile([P, 1], F32)
+        nc.vector.scalar_tensor_tensor(
+            out=thr_sq[:], in0=thr[:], scalar=0.125, in1=thr[:], op0=ALU.mult, op1=ALU.mult
+        )
+
+        x_tiles = {}
+        level2 = {}
+        coeffs = {}
+        codes = {}
+        gates_t = {}
+        gated = {}
+        partial = {}
+
+        def work_tile(shape, name):
+            return sbuf.tile(shape, F32, tag="work", bufs=4, name=name)
+
+        def load(i):
+            x_tiles[i] = sbuf.tile([P, L], BF16, tag="x", bufs=3, name="x_tile")
+            nc.sync.dma_start(out=x_tiles[i][:], in_=x_rows[i * P : (i + 1) * P, :])
+
+        def forward_levels_1_2(i):
+            pairs = x_tiles[i][:].rearrange("p (m two) -> p two m", two=2)
+            level1 = work_tile([P, 2, L // 2], "level1")
+            butterfly(nc, level1[:, 0, :], level1[:, 1, :], pairs[:, 0, :], pairs[:, 1, :])
+            pairs = level1[:].rearrange("p a (m two) -> p a two m", two=2)
+            level2[i] = work_tile([P, 2, 2, L // 4], "level2")
+            butterfly(
+                nc, level2[i][:, :, 0, :], level2[i][:, :, 1, :], pairs[:, :, 0, :], pairs[:, :, 1, :]
+            )
+
+        def forward_level_3(i):
+            pairs = level2[i][:].rearrange("p a b (m two) -> p (a b) two m", two=2)
+            level3 = sbuf.tile([P, NODES // 2, 2, D], F32, tag="coeffs", name="level3")
+            butterfly(nc, level3[:, :, 0, :], level3[:, :, 1, :], pairs[:, :, 0, :], pairs[:, :, 1, :])
+            coeffs[i] = level3[:].rearrange("p a b d -> p (a b) d")
+
+        def quantise_coeffs(i):
+            rounded = sbuf.tile([P, NODES, D], BF16, tag="rounded")
+            nc.scalar.activation(out=rounded[:], in_=coeffs[i], func=ACT.Copy, scale=8.0 ** -0.5)
+            by_word = rounded[:].rearrange("p n (q t) -> p n t q", t=PACK)
+            grouped = sbuf.tile([P, NODES, P, PACK], BF16, tag="grouped", align_bytes=64)
+            for pair in range(NODES // 2):
+                flipped = psum.tile([P, 2, PACK, P], BF16, tag="flipped")
+                for n in range(2):
+                    for t in range(PACK):
+                        nc.tensor.transpose(
+                            flipped[:, n, t, :], by_word[:, 2 * pair + n, t, :], ident_bf16[:]
+                        )
+                nc.scalar.copy(
+                    out=grouped[:, 2 * pair : 2 * pair + 2, :, :],
+                    in_=flipped[:].rearrange("p n t r -> p n r t"),
+                )
+            return grouped
+
+        def multiply(i, grouped):
+            words = sbuf.tile([P, NODES * P], U32, tag="words", align_bytes=64)
+            scales = sbuf.tile([P, NODES * P], U8, tag="scales", align_bytes=64)
+            nc.vector.quantize_mx(
+                out=words[:].bitcast(FP8X4),
+                scales=scales[:],
+                in_=grouped[:].rearrange("p n r t -> p (n r t)"),
+            )
+            gates_t[i] = sbuf.tile([P, E_BLOCKS, NODES * P], F32, tag="gates_t", name="gate_t")
+            for c in range(NODES * P // N_MOVING):
+                cols = slice(c * N_MOVING, (c + 1) * N_MOVING)
+                for k in range(E_BLOCKS):
+                    e_cols = slice(k * P, (k + 1) * P)
+                    z_t = psum.tile([P, N_MOVING], F32, tag="z_t")
+                    nc.tensor.matmul_mx(
+                        out=z_t[:],
+                        lhsT=w_codes[:, e_cols].bitcast(FP8X4),
+                        lhsT_scale=w_scales[:, e_cols],
+                        rhs=words[:, cols].bitcast(FP8X4),
+                        rhs_scale=scales[:, cols],
+                        start=True,
+                        stop=True,
+                    )
+                    nc.scalar.activation(
+                        out=gates_t[i][:, k, cols],
+                        in_=z_t[:],
+                        func=ACT.Sigmoid,
+                        bias=bias[:, k : k + 1],
+                        scale=1.0,
+                    )
+
+        def gate_coeffs(i):
+            product = work_tile([P, NODES, D], "product")
+            squared = work_tile([P, NODES, D], "squared")
+            for n in range(NODES):
+                gate = psum.tile([P, D], F32, tag="gate", bufs=4)
+                for k in range(E_BLOCKS):
+                    nc.tensor.transpose(
+                        gate[:, k * P : (k + 1) * P],
+                        gates_t[i][:, k, n * P : (n + 1) * P],
+                        ident_f32[:],
+                    )
+                nc.vector.scalar_tensor_tensor(
+                    out=product[:, n, :],
+                    in0=gate[:],
+                    scalar=0.125,
+                    in1=coeffs[i][:, n, :],
+                    op0=ALU.mult,
+                    op1=ALU.mult,
+                )
+                nc.scalar.activation(out=squared[:, n, :], in_=product[:, n, :], func=ACT.Square)
+            gated[i] = (product, squared)
+
+        def inverse_levels_1_2(i):
+            product, squared = gated[i]
+            kept = work_tile([P, NODES // 2, 2, D], "kept")
+            nc.vector.scalar_tensor_tensor(
+                out=kept[:].rearrange("p a b d -> p (a b d)"),
+                in0=squared[:].rearrange("p n d -> p (n d)"),
+                scalar=thr_sq[:, 0:1],
+                in1=product[:].rearrange("p n d -> p (n d)"),
+                op0=ALU.is_ge,
+                op1=ALU.mult,
+            )
+            undo3 = work_tile([P, 2, 2, 2, D], "undo3")
+            butterfly(
+                nc,
+                undo3[:, 0, :, :, :].rearrange("p a b d -> p (a b) d"),
+                undo3[:, 1, :, :, :].rearrange("p a b d -> p (a b) d"),
+                kept[:, :, 0, :],
+                kept[:, :, 1, :],
+            )
+            undo2 = work_tile([P, 2, 2, 2, D], "undo2")
+            butterfly(
+                nc, undo2[:, :, 0, :, :], undo2[:, :, 1, :, :], undo3[:, :, :, 0, :], undo3[:, :, :, 1, :]
+            )
+            partial[i] = undo2
+
+        def inverse_level_3_and_store(i):
+            halves = partial[i][:].rearrange("p a b c d -> p (a b) c d")
+            recon = work_tile([P, 4, 2, D], "recon")
+            butterfly(nc, recon[:, :, 0, :], recon[:, :, 1, :], halves[:, :, 0, :], halves[:, :, 1, :])
+            planes = recon[:].rearrange("p a c d -> p (a c) d").rearrange("p (h j) d -> p h d j", h=2)
+            result = sbuf.tile([P, D, 2, 4], F32, tag="result", bufs=2)
+            samples = x_tiles[i][:].rearrange("p (d h j) -> p d h j", h=2, j=4)
+            for h in range(2):
+                nc.vector.tensor_tensor(
+                    out=result[:, :, h, :], in0=planes[:, h, :, :], in1=samples[:, :, h, :], op=ALU.add
+                )
+            nc.sync.dma_start(
+                out=out_rows[i * P : (i + 1) * P, :], in_=result[:].rearrange("p d h j -> p (d h j)")
+            )
+
+        load(0)
+        load(1)
+        with tc.manual_schedule():
+            for i in range(-1, ROW_TILES):
+                ahead = i + 1
+                if ahead + 1 < ROW_TILES and ahead > 0:
+                    load(ahead + 1)
+                if ahead < ROW_TILES:
+                    forward_levels_1_2(ahead)
+                if i >= 0:
+                    gate_coeffs(i)
+                if ahead < ROW_TILES:
+                    forward_level_3(ahead)
+                    grouped = quantise_coeffs(ahead)
+                if i >= 0:
+                    inverse_levels_1_2(i)
+                if ahead < ROW_TILES:
+                    multiply(ahead, grouped)
+                if i >= 0:
+                    inverse_level_3_and_store(i)

@@ -22,12 +22,24 @@ N_MOVING = 512
 ROWS = 64 * 16
 ROW_TILES = ROWS // P
 
+CHUNK_D = P // NODES
+TENSOR_CHUNKS = 12
+BANK_CHUNKS = 4
+TENSOR_L = TENSOR_CHUNKS * P
+TENSOR_D = TENSOR_CHUNKS * CHUNK_D
+VECTOR_L = L - TENSOR_L
+
 FLOPS = 2 * ROWS * NODES * D * D
 
 
 def butterfly(nc, out_sum, out_diff, first, second):
     nc.vector.tensor_tensor(out=out_sum, in0=first, in1=second, op=ALU.add)
     nc.vector.tensor_tensor(out=out_diff, in0=first, in1=second, op=ALU.subtract)
+
+
+def forward_level(nc, out, in_):
+    pairs = in_.rearrange("p g (m two) -> p g two m", two=2)
+    butterfly(nc, out[:, :, 0, :], out[:, :, 1, :], pairs[:, :, 0, :], pairs[:, :, 1, :])
 
 
 def tile_waveletgatednet_kernel(tc, x, W_words, W_scales, b, threshold, out):
@@ -40,10 +52,25 @@ def tile_waveletgatednet_kernel(tc, x, W_words, W_scales, b, threshold, out):
         sbuf = ctx.enter_context(tc.tile_pool(name="sbuf", bufs=1))
         psum = ctx.enter_context(tc.psum_pool(name="psum", bufs=2))
 
+        x_tiles = {}
+
+        def load(i):
+            x_tiles[i] = sbuf.tile([P, L], BF16, tag="x", bufs=4, name="x_tile")
+            nc.sync.dma_start(out=x_tiles[i][:], in_=x_rows[i * P : (i + 1) * P, :])
+
+        load(0)
+
         ident_f32 = const.tile([P, P], F32)
         make_identity(nc, ident_f32[:])
         ident_bf16 = const.tile([P, P], BF16)
         make_identity(nc, ident_bf16[:])
+
+        haar1 = const.tile([P, 1, 2, P // 2], F32)
+        forward_level(nc, haar1[:], ident_f32[:].unsqueeze(1))
+        haar2 = const.tile([P, 2, 2, P // 4], F32)
+        forward_level(nc, haar2[:], haar1[:].rearrange("p g b m -> p (g b) m"))
+        haar = const.tile([P, 4, 2, CHUNK_D], BF16)
+        forward_level(nc, haar[:], haar2[:].rearrange("p g b m -> p (g b) m"))
 
         w_codes = const.tile([P, D], U32, align_bytes=64)
         nc.sync.dma_start(
@@ -75,42 +102,71 @@ def tile_waveletgatednet_kernel(tc, x, W_words, W_scales, b, threshold, out):
             out=thr_sq[:], in0=thr[:], scalar=0.125, in1=thr[:], op0=ALU.mult, op1=ALU.mult
         )
 
-        x_tiles = {}
+        load(1)
+        load(2)
+
+        level1 = {}
         level2 = {}
         coeffs = {}
-        codes = {}
+        grouped = {}
         gates_t = {}
-        gated = {}
-        partial = {}
+        product = {}
+        squared = {}
+        planes = {}
 
         def work_tile(shape, name):
             return sbuf.tile(shape, F32, tag="work", bufs=4, name=name)
 
-        def load(i):
-            x_tiles[i] = sbuf.tile([P, L], BF16, tag="x", bufs=3, name="x_tile")
-            nc.sync.dma_start(out=x_tiles[i][:], in_=x_rows[i * P : (i + 1) * P, :])
 
-        def forward_levels_1_2(i):
-            pairs = x_tiles[i][:].rearrange("p (m two) -> p two m", two=2)
-            level1 = work_tile([P, 2, L // 2], "level1")
-            butterfly(nc, level1[:, 0, :], level1[:, 1, :], pairs[:, 0, :], pairs[:, 1, :])
-            pairs = level1[:].rearrange("p a (m two) -> p a two m", two=2)
-            level2[i] = work_tile([P, 2, 2, L // 4], "level2")
-            butterfly(
-                nc, level2[i][:, :, 0, :], level2[i][:, :, 1, :], pairs[:, :, 0, :], pairs[:, :, 1, :]
-            )
+        def tensor_forward(i):
+            coeffs[i] = sbuf.tile([P, NODES, D], F32, tag="coeffs", bufs=2, name="coeffs_tile")
+            for first in range(0, TENSOR_CHUNKS, BANK_CHUNKS):
+                flipped = psum.tile([P, BANK_CHUNKS, P], BF16, tag="flipped")
+                for c in range(BANK_CHUNKS):
+                    nc.tensor.transpose(
+                        flipped[:, c, :],
+                        x_tiles[i][:, (first + c) * P : (first + c + 1) * P],
+                        ident_bf16[:],
+                    )
+                x_t = sbuf.tile([P, BANK_CHUNKS, P], BF16, tag="x_t", bufs=2)
+                nc.scalar.copy(out=x_t[:], in_=flipped[:])
+                summed = psum.tile([P, BANK_CHUNKS, NODES, CHUNK_D], F32, tag="z_t")
+                for c in range(BANK_CHUNKS):
+                    nc.tensor.matmul(
+                        out=summed[:, c, :, :].rearrange("p n d -> p (n d)"),
+                        lhsT=x_t[:, c, :],
+                        rhs=haar[:].rearrange("p g b d -> p (g b d)"),
+                        start=True,
+                        stop=True,
+                    )
+                d_range = slice(first * CHUNK_D, (first + BANK_CHUNKS) * CHUNK_D)
+                nc.scalar.copy(
+                    out=coeffs[i][:, :, d_range].rearrange("p n (c d) -> p n c d", c=BANK_CHUNKS),
+                    in_=summed[:].rearrange("p c n d -> p n c d"),
+                )
+
+        def forward_level_1(i):
+            level1[i] = work_tile([P, 1, 2, VECTOR_L // 2], "level1_tile")
+            forward_level(nc, level1[i][:], x_tiles[i][:, TENSOR_L:L].unsqueeze(1))
+
+        def forward_level_2(i):
+            level2[i] = sbuf.tile([P, 2, 2, VECTOR_L // 4], F32, tag="level2", name="level2_tile")
+            forward_level(nc, level2[i][:], level1[i][:].rearrange("p g b m -> p (g b) m"))
 
         def forward_level_3(i):
-            pairs = level2[i][:].rearrange("p a b (m two) -> p (a b) two m", two=2)
-            level3 = sbuf.tile([P, NODES // 2, 2, D], F32, tag="coeffs", name="level3")
-            butterfly(nc, level3[:, :, 0, :], level3[:, :, 1, :], pairs[:, :, 0, :], pairs[:, :, 1, :])
-            coeffs[i] = level3[:].rearrange("p a b d -> p (a b) d")
+            forward_level(
+                nc,
+                coeffs[i][:, :, TENSOR_D:D].rearrange("p (g b) d -> p g b d", b=2),
+                level2[i][:].rearrange("p g b m -> p (g b) m"),
+            )
 
-        def quantise_coeffs(i):
+        def round_and_transpose(i):
             rounded = sbuf.tile([P, NODES, D], BF16, tag="rounded")
-            nc.scalar.activation(out=rounded[:], in_=coeffs[i], func=ACT.Copy, scale=8.0 ** -0.5)
+            nc.scalar.activation(out=rounded[:], in_=coeffs[i][:], func=ACT.Copy, scale=8.0 ** -0.5)
             by_word = rounded[:].rearrange("p n (q t) -> p n t q", t=PACK)
-            grouped = sbuf.tile([P, NODES, P, PACK], BF16, tag="grouped", align_bytes=64)
+            grouped[i] = sbuf.tile(
+                [P, NODES, P, PACK], BF16, tag="grouped", align_bytes=64, name="grouped_tile"
+            )
             for pair in range(NODES // 2):
                 flipped = psum.tile([P, 2, PACK, P], BF16, tag="flipped")
                 for n in range(2):
@@ -119,18 +175,17 @@ def tile_waveletgatednet_kernel(tc, x, W_words, W_scales, b, threshold, out):
                             flipped[:, n, t, :], by_word[:, 2 * pair + n, t, :], ident_bf16[:]
                         )
                 nc.scalar.copy(
-                    out=grouped[:, 2 * pair : 2 * pair + 2, :, :],
+                    out=grouped[i][:, 2 * pair : 2 * pair + 2, :, :],
                     in_=flipped[:].rearrange("p n t r -> p n r t"),
                 )
-            return grouped
 
-        def multiply(i, grouped):
+        def multiply(i):
             words = sbuf.tile([P, NODES * P], U32, tag="words", align_bytes=64)
             scales = sbuf.tile([P, NODES * P], U8, tag="scales", align_bytes=64)
             nc.vector.quantize_mx(
                 out=words[:].bitcast(FP8X4),
                 scales=scales[:],
-                in_=grouped[:].rearrange("p n r t -> p (n r t)"),
+                in_=grouped[i][:].rearrange("p n r t -> p (n r t)"),
             )
             gates_t[i] = sbuf.tile([P, E_BLOCKS, NODES * P], F32, tag="gates_t", name="gate_t")
             for c in range(NODES * P // N_MOVING):
@@ -156,8 +211,8 @@ def tile_waveletgatednet_kernel(tc, x, W_words, W_scales, b, threshold, out):
                     )
 
         def gate_coeffs(i):
-            product = work_tile([P, NODES, D], "product")
-            squared = work_tile([P, NODES, D], "squared")
+            product[i] = work_tile([P, NODES, D], "product_tile")
+            squared[i] = work_tile([P, NODES, D], "squared_tile")
             for n in range(NODES):
                 gate = psum.tile([P, D], F32, tag="gate", bufs=4)
                 for k in range(E_BLOCKS):
@@ -167,73 +222,82 @@ def tile_waveletgatednet_kernel(tc, x, W_words, W_scales, b, threshold, out):
                         ident_f32[:],
                     )
                 nc.vector.scalar_tensor_tensor(
-                    out=product[:, n, :],
+                    out=product[i][:, n, :],
                     in0=gate[:],
                     scalar=0.125,
                     in1=coeffs[i][:, n, :],
                     op0=ALU.mult,
                     op1=ALU.mult,
                 )
-                nc.scalar.activation(out=squared[:, n, :], in_=product[:, n, :], func=ACT.Square)
-            gated[i] = (product, squared)
+                nc.scalar.activation(
+                    out=squared[i][:, n, :], in_=product[i][:, n, :], func=ACT.Square
+                )
 
-        def inverse_levels_1_2(i):
-            product, squared = gated[i]
-            kept = work_tile([P, NODES // 2, 2, D], "kept")
+        def keep_large(i):
+            kept = work_tile([P, NODES, D], "kept")
             nc.vector.scalar_tensor_tensor(
-                out=kept[:].rearrange("p a b d -> p (a b d)"),
-                in0=squared[:].rearrange("p n d -> p (n d)"),
+                out=kept[:].rearrange("p n d -> p (n d)"),
+                in0=squared[i][:].rearrange("p n d -> p (n d)"),
                 scalar=thr_sq[:, 0:1],
-                in1=product[:].rearrange("p n d -> p (n d)"),
+                in1=product[i][:].rearrange("p n d -> p (n d)"),
                 op0=ALU.is_ge,
                 op1=ALU.mult,
             )
-            undo3 = work_tile([P, 2, 2, 2, D], "undo3")
-            butterfly(
-                nc,
-                undo3[:, 0, :, :, :].rearrange("p a b d -> p (a b) d"),
-                undo3[:, 1, :, :, :].rearrange("p a b d -> p (a b) d"),
-                kept[:, :, 0, :],
-                kept[:, :, 1, :],
-            )
-            undo2 = work_tile([P, 2, 2, 2, D], "undo2")
-            butterfly(
-                nc, undo2[:, :, 0, :, :], undo2[:, :, 1, :, :], undo3[:, :, :, 0, :], undo3[:, :, :, 1, :]
-            )
-            partial[i] = undo2
+            planes[i] = kept
 
-        def inverse_level_3_and_store(i):
-            halves = partial[i][:].rearrange("p a b c d -> p (a b) c d")
-            recon = work_tile([P, 4, 2, D], "recon")
-            butterfly(nc, recon[:, :, 0, :], recon[:, :, 1, :], halves[:, :, 0, :], halves[:, :, 1, :])
-            planes = recon[:].rearrange("p a c d -> p (a c) d").rearrange("p (h j) d -> p h d j", h=2)
-            result = sbuf.tile([P, D, 2, 4], F32, tag="result", bufs=2)
+        def inverse_level(i, level):
+            outer = 2 ** level
+            before = planes[i][:].rearrange("p (o b n) d -> p o b (n d)", o=outer, b=2)
+            planes[i] = work_tile([P, NODES, D], "after")
+            after = planes[i][:].rearrange("p (j o n) d -> p j o (n d)", j=2, o=outer)
+            butterfly(
+                nc, after[:, 0, :, :], after[:, 1, :, :], before[:, :, 0, :], before[:, :, 1, :]
+            )
+
+        def add_residual_and_store(i):
+            by_sample = planes[i][:].rearrange("p (h j) d -> p h d j", h=2)
+            result = sbuf.tile([P, D, 2, 4], F32, tag="result")
             samples = x_tiles[i][:].rearrange("p (d h j) -> p d h j", h=2, j=4)
             for h in range(2):
                 nc.vector.tensor_tensor(
-                    out=result[:, :, h, :], in0=planes[:, h, :, :], in1=samples[:, :, h, :], op=ALU.add
+                    out=result[:, :, h, :],
+                    in0=by_sample[:, h, :, :],
+                    in1=samples[:, :, h, :],
+                    op=ALU.add,
                 )
             nc.sync.dma_start(
                 out=out_rows[i * P : (i + 1) * P, :], in_=result[:].rearrange("p d h j -> p (d h j)")
             )
 
-        load(0)
-        load(1)
         with tc.manual_schedule():
-            for i in range(-1, ROW_TILES):
-                ahead = i + 1
-                if ahead + 1 < ROW_TILES and ahead > 0:
-                    load(ahead + 1)
-                if ahead < ROW_TILES:
-                    forward_levels_1_2(ahead)
-                if i >= 0:
-                    gate_coeffs(i)
-                if ahead < ROW_TILES:
-                    forward_level_3(ahead)
-                    grouped = quantise_coeffs(ahead)
-                if i >= 0:
-                    inverse_levels_1_2(i)
-                if ahead < ROW_TILES:
-                    multiply(ahead, grouped)
-                if i >= 0:
-                    inverse_level_3_and_store(i)
+            tensor_forward(0)
+            forward_level_1(0)
+            forward_level_2(0)
+            for back in range(-1, ROW_TILES):
+                mid = back + 1
+                front = back + 2
+                if front + 1 < ROW_TILES and back >= 0:
+                    load(front + 1)
+                if back >= 0:
+                    gate_coeffs(back)
+                if mid < ROW_TILES:
+                    forward_level_3(mid)
+                if front < ROW_TILES:
+                    tensor_forward(front)
+                if mid < ROW_TILES:
+                    round_and_transpose(mid)
+                if back >= 0:
+                    keep_large(back)
+                if front < ROW_TILES:
+                    forward_level_1(front)
+                if back >= 0:
+                    inverse_level(back, 0)
+                if front < ROW_TILES:
+                    forward_level_2(front)
+                if back >= 0:
+                    inverse_level(back, 1)
+                if mid < ROW_TILES:
+                    multiply(mid)
+                if back >= 0:
+                    inverse_level(back, 2)
+                    add_residual_and_store(back)

@@ -21,6 +21,8 @@ E_BLOCKS = D // P
 N_MOVING = 512
 ROWS = 64 * 16
 ROW_TILES = ROWS // P
+UNITS = ROW_TILES * E_BLOCKS
+PAIRS = NODES // 2
 
 CHUNK_D = P // NODES
 TENSOR_CHUNKS = 12
@@ -102,51 +104,55 @@ def tile_waveletgatednet_kernel(tc, x, W_words, W_scales, b, threshold, out):
             out=thr_sq[:], in0=thr[:], scalar=0.125, in1=thr[:], op0=ALU.mult, op1=ALU.mult
         )
 
-        load(1)
-        load(2)
-
         level1 = {}
         level2 = {}
         coeffs = {}
         grouped = {}
+        words = {}
+        scales = {}
         gates_t = {}
+        coeffs_t = {}
         product = {}
         squared = {}
-        planes = {}
+        kept = {}
+        half_back = {}
+        negated = {}
+        back = {}
 
-        def work_tile(shape, name):
-            return sbuf.tile(shape, F32, tag="work", bufs=4, name=name)
+        def unit_tile(tag, bufs):
+            return sbuf.tile([P, NODES, P], F32, tag=tag, bufs=bufs, name=tag + "_tile")
 
 
-        def tensor_forward(i):
-            coeffs[i] = sbuf.tile([P, NODES, D], F32, tag="coeffs", bufs=2, name="coeffs_tile")
-            for first in range(0, TENSOR_CHUNKS, BANK_CHUNKS):
-                flipped = psum.tile([P, BANK_CHUNKS, P], BF16, tag="flipped")
-                for c in range(BANK_CHUNKS):
-                    nc.tensor.transpose(
-                        flipped[:, c, :],
-                        x_tiles[i][:, (first + c) * P : (first + c + 1) * P],
-                        ident_bf16[:],
-                    )
-                x_t = sbuf.tile([P, BANK_CHUNKS, P], BF16, tag="x_t", bufs=2)
-                nc.scalar.copy(out=x_t[:], in_=flipped[:])
-                summed = psum.tile([P, BANK_CHUNKS, NODES, CHUNK_D], F32, tag="z_t")
-                for c in range(BANK_CHUNKS):
-                    nc.tensor.matmul(
-                        out=summed[:, c, :, :].rearrange("p n d -> p (n d)"),
-                        lhsT=x_t[:, c, :],
-                        rhs=haar[:].rearrange("p g b d -> p (g b d)"),
-                        start=True,
-                        stop=True,
-                    )
-                d_range = slice(first * CHUNK_D, (first + BANK_CHUNKS) * CHUNK_D)
-                nc.scalar.copy(
-                    out=coeffs[i][:, :, d_range].rearrange("p n (c d) -> p n c d", c=BANK_CHUNKS),
-                    in_=summed[:].rearrange("p c n d -> p n c d"),
+        def tensor_forward(i, group):
+            if group == 0:
+                coeffs[i] = sbuf.tile([P, NODES, D], F32, tag="coeffs", bufs=3, name="coeffs_tile")
+            first = group * BANK_CHUNKS
+            flipped = psum.tile([P, BANK_CHUNKS, P], BF16, tag="flipped")
+            for c in range(BANK_CHUNKS):
+                nc.tensor.transpose(
+                    flipped[:, c, :],
+                    x_tiles[i][:, (first + c) * P : (first + c + 1) * P],
+                    ident_bf16[:],
                 )
+            x_t = sbuf.tile([P, BANK_CHUNKS, P], BF16, tag="x_t", bufs=2)
+            nc.scalar.copy(out=x_t[:], in_=flipped[:])
+            summed = psum.tile([P, BANK_CHUNKS, NODES, CHUNK_D], F32, tag="z_t")
+            for c in range(BANK_CHUNKS):
+                nc.tensor.matmul(
+                    out=summed[:, c, :, :].rearrange("p n d -> p (n d)"),
+                    lhsT=x_t[:, c, :],
+                    rhs=haar[:].rearrange("p g b d -> p (g b d)"),
+                    start=True,
+                    stop=True,
+                )
+            d_range = slice(first * CHUNK_D, (first + BANK_CHUNKS) * CHUNK_D)
+            nc.scalar.copy(
+                out=coeffs[i][:, :, d_range].rearrange("p n (c d) -> p n c d", c=BANK_CHUNKS),
+                in_=summed[:].rearrange("p c n d -> p n c d"),
+            )
 
         def forward_level_1(i):
-            level1[i] = work_tile([P, 1, 2, VECTOR_L // 2], "level1_tile")
+            level1[i] = sbuf.tile([P, 1, 2, VECTOR_L // 2], F32, tag="level1", name="level1_tile")
             forward_level(nc, level1[i][:], x_tiles[i][:, TENSOR_L:L].unsqueeze(1))
 
         def forward_level_2(i):
@@ -160,144 +166,183 @@ def tile_waveletgatednet_kernel(tc, x, W_words, W_scales, b, threshold, out):
                 level2[i][:].rearrange("p g b m -> p (g b) m"),
             )
 
-        def round_and_transpose(i):
-            rounded = sbuf.tile([P, NODES, D], BF16, tag="rounded")
-            nc.scalar.activation(out=rounded[:], in_=coeffs[i][:], func=ACT.Copy, scale=8.0 ** -0.5)
-            by_word = rounded[:].rearrange("p n (q t) -> p n t q", t=PACK)
-            grouped[i] = sbuf.tile(
-                [P, NODES, P, PACK], BF16, tag="grouped", align_bytes=64, name="grouped_tile"
-            )
-            for pair in range(NODES // 2):
-                flipped = psum.tile([P, 2, PACK, P], BF16, tag="flipped")
-                for n in range(2):
-                    for t in range(PACK):
-                        nc.tensor.transpose(
-                            flipped[:, n, t, :], by_word[:, 2 * pair + n, t, :], ident_bf16[:]
-                        )
-                nc.scalar.copy(
-                    out=grouped[i][:, 2 * pair : 2 * pair + 2, :, :],
-                    in_=flipped[:].rearrange("p n t r -> p n r t"),
+        def round_and_transpose(i, pair):
+            if pair == 0:
+                grouped[i] = sbuf.tile(
+                    [P, NODES, P, PACK], BF16, tag="grouped", bufs=2, align_bytes=64, name="grouped_tile"
+                )
+            for n in (2 * pair, 2 * pair + 1):
+                by_word = coeffs[i][:, n, :].rearrange("p (q t) -> p t q", t=PACK)
+                flipped = psum.tile([P, PACK, P], F32, tag="flipped")
+                for t in range(PACK):
+                    nc.tensor.transpose(flipped[:, t, :], by_word[:, t, :], ident_f32[:])
+                nc.scalar.activation(
+                    out=grouped[i][:, n, :, :],
+                    in_=flipped[:].rearrange("p t r -> p r t"),
+                    func=ACT.Copy,
+                    scale=8.0 ** -0.5,
                 )
 
-        def multiply(i):
-            words = sbuf.tile([P, NODES * P], U32, tag="words", align_bytes=64)
-            scales = sbuf.tile([P, NODES * P], U8, tag="scales", align_bytes=64)
+        def quantise(i):
+            words[i] = sbuf.tile([P, NODES * P], U32, tag="words", align_bytes=64, name="words_tile")
+            scales[i] = sbuf.tile([P, NODES * P], U8, tag="scales", align_bytes=64, name="scales_tile")
             nc.vector.quantize_mx(
-                out=words[:].bitcast(FP8X4),
-                scales=scales[:],
+                out=words[i][:].bitcast(FP8X4),
+                scales=scales[i][:],
                 in_=grouped[i][:].rearrange("p n r t -> p (n r t)"),
             )
-            gates_t[i] = sbuf.tile([P, E_BLOCKS, NODES * P], F32, tag="gates_t", name="gate_t")
+
+
+        def multiply(u):
+            i, k = divmod(u, E_BLOCKS)
+            e_cols = slice(k * P, (k + 1) * P)
+            gates_t[u] = unit_tile("gates_t", 2)
             for c in range(NODES * P // N_MOVING):
                 cols = slice(c * N_MOVING, (c + 1) * N_MOVING)
-                for k in range(E_BLOCKS):
-                    e_cols = slice(k * P, (k + 1) * P)
-                    z_t = psum.tile([P, N_MOVING], F32, tag="z_t")
-                    nc.tensor.matmul_mx(
-                        out=z_t[:],
-                        lhsT=w_codes[:, e_cols].bitcast(FP8X4),
-                        lhsT_scale=w_scales[:, e_cols],
-                        rhs=words[:, cols].bitcast(FP8X4),
-                        rhs_scale=scales[:, cols],
-                        start=True,
-                        stop=True,
-                    )
-                    nc.scalar.activation(
-                        out=gates_t[i][:, k, cols],
-                        in_=z_t[:],
-                        func=ACT.Sigmoid,
-                        bias=bias[:, k : k + 1],
-                        scale=1.0,
-                    )
+                z_t = psum.tile([P, N_MOVING], F32, tag="z_t")
+                nc.tensor.matmul_mx(
+                    out=z_t[:],
+                    lhsT=w_codes[:, e_cols].bitcast(FP8X4),
+                    lhsT_scale=w_scales[:, e_cols],
+                    rhs=words[i][:, cols].bitcast(FP8X4),
+                    rhs_scale=scales[i][:, cols],
+                    start=True,
+                    stop=True,
+                )
+                nc.scalar.activation(
+                    out=gates_t[u][:].rearrange("p n r -> p (n r)")[:, cols],
+                    in_=z_t[:],
+                    func=ACT.Sigmoid,
+                    bias=bias[:, k : k + 1],
+                    scale=1.0,
+                )
 
-        def gate_coeffs(i):
-            product[i] = work_tile([P, NODES, D], "product_tile")
-            squared[i] = work_tile([P, NODES, D], "squared_tile")
-            for n in range(NODES):
-                gate = psum.tile([P, D], F32, tag="gate", bufs=4)
-                for k in range(E_BLOCKS):
+        def transpose_coeffs(u):
+            i, k = divmod(u, E_BLOCKS)
+            coeffs_t[u] = []
+            for half in range(2):
+                bank = psum.tile([P, NODES // 2, P], F32, tag="coeffs_t", name="coeffs_t_bank")
+                for n in range(NODES // 2):
                     nc.tensor.transpose(
-                        gate[:, k * P : (k + 1) * P],
-                        gates_t[i][:, k, n * P : (n + 1) * P],
+                        bank[:, n, :],
+                        coeffs[i][:, half * (NODES // 2) + n, k * P : (k + 1) * P],
                         ident_f32[:],
                     )
+                coeffs_t[u].append(bank)
+
+        def gate_coeffs(u):
+            product[u] = unit_tile("product", 2)
+            for half in range(2):
+                nodes = slice(half * (NODES // 2), (half + 1) * (NODES // 2))
                 nc.vector.scalar_tensor_tensor(
-                    out=product[i][:, n, :],
-                    in0=gate[:],
+                    out=product[u][:, nodes, :],
+                    in0=coeffs_t[u][half][:],
                     scalar=0.125,
-                    in1=coeffs[i][:, n, :],
+                    in1=gates_t[u][:, nodes, :],
                     op0=ALU.mult,
                     op1=ALU.mult,
                 )
-                nc.scalar.activation(
-                    out=squared[i][:, n, :], in_=product[i][:, n, :], func=ACT.Square
-                )
+            squared[u] = unit_tile("squared", 2)
+            nc.scalar.activation(out=squared[u][:], in_=product[u][:], func=ACT.Square)
 
-        def keep_large(i):
-            kept = work_tile([P, NODES, D], "kept")
+        def keep_large(u):
+            kept[u] = unit_tile("kept", 2)
             nc.vector.scalar_tensor_tensor(
-                out=kept[:].rearrange("p n d -> p (n d)"),
-                in0=squared[i][:].rearrange("p n d -> p (n d)"),
+                out=kept[u][:],
+                in0=squared[u][:],
                 scalar=thr_sq[:, 0:1],
-                in1=product[i][:].rearrange("p n d -> p (n d)"),
+                in1=product[u][:],
                 op0=ALU.is_ge,
                 op1=ALU.mult,
             )
-            planes[i] = kept
 
-        def inverse_level(i, level):
-            outer = 2 ** level
-            before = planes[i][:].rearrange("p (o b n) d -> p o b (n d)", o=outer, b=2)
-            planes[i] = work_tile([P, NODES, D], "after")
-            after = planes[i][:].rearrange("p (j o n) d -> p j o (n d)", j=2, o=outer)
+
+        def inverse_level_n1(u):
+            half_back[u] = unit_tile("half_back", 3)
+            low, high = slice(0, NODES // 2), slice(NODES // 2, NODES)
             butterfly(
-                nc, after[:, 0, :, :], after[:, 1, :, :], before[:, :, 0, :], before[:, :, 1, :]
+                nc, half_back[u][:, low, :], half_back[u][:, high, :], kept[u][:, low, :], kept[u][:, high, :]
             )
 
-        def add_residual_and_store(i):
-            by_sample = planes[i][:].rearrange("p (h j) d -> p h d j", h=2)
-            result = sbuf.tile([P, D, 2, 4], F32, tag="result")
-            samples = x_tiles[i][:].rearrange("p (d h j) -> p d h j", h=2, j=4)
-            for h in range(2):
+        def negate(u):
+            negated[u] = unit_tile("negated", 3)
+            nc.scalar.mul(
+                out=negated[u][:].rearrange("p (j m) r -> p j m r", j=2)[:, :, 1:4, :],
+                in_=half_back[u][:].rearrange("p (j m) r -> p j m r", j=2)[:, :, 1:4, :],
+                mul=-1.0,
+            )
+
+        def inverse_levels_n2_n3(u):
+            back[u] = []
+            for j2 in range(2):
+                bank = psum.tile([P, 4, P], F32, tag="back", name="back_bank")
+                for j1 in range(2):
+                    for j0 in range(2):
+                        for n2 in range(2):
+                            for n3 in range(2):
+                                source = negated[u] if (n2 * j1 + n3 * j2) % 2 else half_back[u]
+                                nc.tensor.matmul(
+                                    out=bank[:, 2 * j1 + j0, :],
+                                    lhsT=source[:, 4 * j0 + 2 * n2 + n3, :],
+                                    rhs=ident_f32[:],
+                                    is_transpose=True,
+                                    start=(n2 == 0 and n3 == 0),
+                                    stop=(n2 == 1 and n3 == 1),
+                                )
+                back[u].append(bank)
+
+        def add_residual_and_store(u):
+            i, k = divmod(u, E_BLOCKS)
+            unit_samples = slice(k * P * NODES, (k + 1) * P * NODES)
+            samples = x_tiles[i][:, unit_samples].rearrange("p (d h j) -> p d h j", h=2, j=4)
+            result = sbuf.tile([P, P, 2, 4], F32, tag="result", bufs=3)
+            for j2 in range(2):
                 nc.vector.tensor_tensor(
-                    out=result[:, :, h, :],
-                    in0=by_sample[:, h, :, :],
-                    in1=samples[:, :, h, :],
+                    out=result[:, :, j2, :],
+                    in0=back[u][j2][:].rearrange("p j d -> p d j"),
+                    in1=samples[:, :, j2, :],
                     op=ALU.add,
                 )
             nc.sync.dma_start(
-                out=out_rows[i * P : (i + 1) * P, :], in_=result[:].rearrange("p d h j -> p (d h j)")
+                out=out_rows[i * P : (i + 1) * P, unit_samples],
+                in_=result[:].rearrange("p d h j -> p (d h j)"),
             )
 
+        def is_tile(i):
+            return 0 <= i < ROW_TILES
+
+        def is_unit(u):
+            return 0 <= u < UNITS
+
         with tc.manual_schedule():
-            tensor_forward(0)
-            forward_level_1(0)
-            forward_level_2(0)
-            for back in range(-1, ROW_TILES):
-                mid = back + 1
-                front = back + 2
-                if front + 1 < ROW_TILES and back >= 0:
-                    load(front + 1)
-                if back >= 0:
-                    gate_coeffs(back)
-                if mid < ROW_TILES:
-                    forward_level_3(mid)
-                if front < ROW_TILES:
-                    tensor_forward(front)
-                if mid < ROW_TILES:
-                    round_and_transpose(mid)
-                if back >= 0:
-                    keep_large(back)
-                if front < ROW_TILES:
-                    forward_level_1(front)
-                if back >= 0:
-                    inverse_level(back, 0)
-                if front < ROW_TILES:
-                    forward_level_2(front)
-                if back >= 0:
-                    inverse_level(back, 1)
-                if mid < ROW_TILES:
-                    multiply(mid)
-                if back >= 0:
-                    inverse_level(back, 2)
-                    add_residual_and_store(back)
+            for j in range(-2 * E_BLOCKS, UNITS + 2):
+                i, k = divmod(j, E_BLOCKS)
+                if is_unit(j - 1):
+                    negate(j - 1)
+                if is_unit(j):
+                    gate_coeffs(j)
+                if k == 0 and is_tile(i + 2):
+                    forward_level_1(i + 2)
+                if k == 1 and is_tile(i + 2):
+                    forward_level_2(i + 2)
+                if k == 2 and is_tile(i + 2):
+                    forward_level_3(i + 2)
+                if k == 3 and is_tile(i + 1):
+                    quantise(i + 1)
+                if is_unit(j + 1):
+                    multiply(j + 1)
+                    transpose_coeffs(j + 1)
+                if is_tile((j + 5) // PAIRS):
+                    round_and_transpose((j + 5) // PAIRS, (j + 5) % PAIRS)
+                if k < TENSOR_CHUNKS // BANK_CHUNKS and is_tile(i + 2):
+                    tensor_forward(i + 2, k)
+                if is_unit(j):
+                    keep_large(j)
+                if is_unit(j - 2):
+                    add_residual_and_store(j - 2)
+                if k == 1 and is_tile(i + 3):
+                    load(i + 3)
+                if is_unit(j - 1):
+                    inverse_levels_n2_n3(j - 1)
+                if is_unit(j):
+                    inverse_level_n1(j)

@@ -115,7 +115,8 @@ def tile_waveletgatednet_kernel(tc, x, W_words, W_scales, b, threshold, out):
         product = {}
         squared = {}
         kept = {}
-        half_back = {}
+        after_n1 = {}
+        after_n2 = {}
         negated = {}
         back = {}
 
@@ -258,37 +259,50 @@ def tile_waveletgatednet_kernel(tc, x, W_words, W_scales, b, threshold, out):
 
 
         def inverse_level_n1(u):
-            half_back[u] = unit_tile("half_back", 3)
+            after_n1[u] = unit_tile("after_n1", 2)
             low, high = slice(0, NODES // 2), slice(NODES // 2, NODES)
             butterfly(
-                nc, half_back[u][:, low, :], half_back[u][:, high, :], kept[u][:, low, :], kept[u][:, high, :]
+                nc, after_n1[u][:, low, :], after_n1[u][:, high, :], kept[u][:, low, :], kept[u][:, high, :]
+            )
+
+        def inverse_level_n2(u):
+            before = after_n1[u][:].rearrange("p (a b c) r -> p a b (c r)", a=2, b=2)
+            after_n2[u] = unit_tile("after_n2", 3)
+            after = after_n2[u][:].rearrange("p (a b c) r -> p a b (c r)", a=2, b=2)
+            butterfly(
+                nc, after[:, 0, :, :], after[:, 1, :, :], before[:, :, 0, :], before[:, :, 1, :]
             )
 
         def negate(u):
             negated[u] = unit_tile("negated", 3)
             nc.scalar.mul(
-                out=negated[u][:].rearrange("p (j m) r -> p j m r", j=2)[:, :, 1:4, :],
-                in_=half_back[u][:].rearrange("p (j m) r -> p j m r", j=2)[:, :, 1:4, :],
+                out=negated[u][:].rearrange("p (m c) r -> p m c r", c=2)[:, :, 1, :],
+                in_=after_n2[u][:].rearrange("p (m c) r -> p m c r", c=2)[:, :, 1, :],
                 mul=-1.0,
             )
 
-        def inverse_levels_n2_n3(u):
+        def inverse_level_n3(u):
             back[u] = []
             for j2 in range(2):
+                second = negated[u] if j2 else after_n2[u]
                 bank = psum.tile([P, 4, P], F32, tag="back", name="back_bank")
-                for j1 in range(2):
-                    for j0 in range(2):
-                        for n2 in range(2):
-                            for n3 in range(2):
-                                source = negated[u] if (n2 * j1 + n3 * j2) % 2 else half_back[u]
-                                nc.tensor.matmul(
-                                    out=bank[:, 2 * j1 + j0, :],
-                                    lhsT=source[:, 4 * j0 + 2 * n2 + n3, :],
-                                    rhs=ident_f32[:],
-                                    is_transpose=True,
-                                    start=(n2 == 0 and n3 == 0),
-                                    stop=(n2 == 1 and n3 == 1),
-                                )
+                for m in range(4):
+                    nc.tensor.matmul(
+                        out=bank[:, m, :],
+                        lhsT=after_n2[u][:, 2 * m, :],
+                        rhs=ident_f32[:],
+                        is_transpose=True,
+                        start=True,
+                        stop=False,
+                    )
+                    nc.tensor.matmul(
+                        out=bank[:, m, :],
+                        lhsT=second[:, 2 * m + 1, :],
+                        rhs=ident_f32[:],
+                        is_transpose=True,
+                        start=False,
+                        stop=True,
+                    )
                 back[u].append(bank)
 
         def add_residual_and_store(u):
@@ -317,8 +331,6 @@ def tile_waveletgatednet_kernel(tc, x, W_words, W_scales, b, threshold, out):
         with tc.manual_schedule():
             for j in range(-2 * E_BLOCKS, UNITS + 2):
                 i, k = divmod(j, E_BLOCKS)
-                if is_unit(j - 1):
-                    negate(j - 1)
                 if is_unit(j):
                     gate_coeffs(j)
                 if k == 0 and is_tile(i + 2):
@@ -343,6 +355,8 @@ def tile_waveletgatednet_kernel(tc, x, W_words, W_scales, b, threshold, out):
                 if k == 1 and is_tile(i + 3):
                     load(i + 3)
                 if is_unit(j - 1):
-                    inverse_levels_n2_n3(j - 1)
+                    inverse_level_n2(j - 1)
+                    negate(j - 1)
+                    inverse_level_n3(j - 1)
                 if is_unit(j):
                     inverse_level_n1(j)

@@ -39,6 +39,17 @@ def butterfly(nc, out_sum, out_diff, first, second):
     nc.vector.tensor_tensor(out=out_diff, in0=first, in1=second, op=ALU.subtract)
 
 
+def shared_butterfly(nc, out_sum, out_diff, first, second):
+    half = out_diff.shape[1] // 2
+    nc.vector.tensor_tensor(out=out_sum, in0=first, in1=second, op=ALU.add)
+    nc.vector.tensor_tensor(
+        out=out_diff[:, :half, :], in0=first[:, :half, :], in1=second[:, :half, :], op=ALU.subtract
+    )
+    nc.gpsimd.tensor_tensor(
+        out=out_diff[:, half:, :], in0=first[:, half:, :], in1=second[:, half:, :], op=ALU.subtract
+    )
+
+
 def forward_level(nc, out, in_):
     pairs = in_.rearrange("p g (m two) -> p g two m", two=2)
     butterfly(nc, out[:, :, 0, :], out[:, :, 1, :], pairs[:, :, 0, :], pairs[:, :, 1, :])
@@ -261,7 +272,7 @@ def tile_waveletgatednet_kernel(tc, x, W_words, W_scales, b, threshold, out):
         def inverse_level_n1(u):
             after_n1[u] = unit_tile("after_n1", 2)
             low, high = slice(0, NODES // 2), slice(NODES // 2, NODES)
-            butterfly(
+            shared_butterfly(
                 nc, after_n1[u][:, low, :], after_n1[u][:, high, :], kept[u][:, low, :], kept[u][:, high, :]
             )
 
@@ -269,7 +280,7 @@ def tile_waveletgatednet_kernel(tc, x, W_words, W_scales, b, threshold, out):
             before = after_n1[u][:].rearrange("p (a b c) r -> p a b (c r)", a=2, b=2)
             after_n2[u] = unit_tile("after_n2", 3)
             after = after_n2[u][:].rearrange("p (a b c) r -> p a b (c r)", a=2, b=2)
-            butterfly(
+            shared_butterfly(
                 nc, after[:, 0, :, :], after[:, 1, :, :], before[:, :, 0, :], before[:, :, 1, :]
             )
 

@@ -39,17 +39,6 @@ def butterfly(nc, out_sum, out_diff, first, second):
     nc.vector.tensor_tensor(out=out_diff, in0=first, in1=second, op=ALU.subtract)
 
 
-def shared_butterfly(nc, out_sum, out_diff, first, second):
-    half = out_diff.shape[1] // 2
-    nc.vector.tensor_tensor(out=out_sum, in0=first, in1=second, op=ALU.add)
-    nc.vector.tensor_tensor(
-        out=out_diff[:, :half, :], in0=first[:, :half, :], in1=second[:, :half, :], op=ALU.subtract
-    )
-    nc.gpsimd.tensor_tensor(
-        out=out_diff[:, half:, :], in0=first[:, half:, :], in1=second[:, half:, :], op=ALU.subtract
-    )
-
-
 def forward_level(nc, out, in_):
     pairs = in_.rearrange("p g (m two) -> p g two m", two=2)
     butterfly(nc, out[:, :, 0, :], out[:, :, 1, :], pairs[:, :, 0, :], pairs[:, :, 1, :])
@@ -68,7 +57,7 @@ def tile_waveletgatednet_kernel(tc, x, W_words, W_scales, b, threshold, out):
         x_tiles = {}
 
         def load(i):
-            x_tiles[i] = sbuf.tile([P, L], BF16, tag="x", bufs=4, name="x_tile")
+            x_tiles[i] = sbuf.tile([P, L], BF16, tag="x", bufs=5, name="x_tile")
             nc.sync.dma_start(out=x_tiles[i][:], in_=x_rows[i * P : (i + 1) * P, :])
 
         load(0)
@@ -196,8 +185,12 @@ def tile_waveletgatednet_kernel(tc, x, W_words, W_scales, b, threshold, out):
                 )
 
         def quantise(i):
-            words[i] = sbuf.tile([P, NODES * P], U32, tag="words", align_bytes=64, name="words_tile")
-            scales[i] = sbuf.tile([P, NODES * P], U8, tag="scales", align_bytes=64, name="scales_tile")
+            words[i] = sbuf.tile(
+                [P, NODES * P], U32, tag="words", bufs=2, align_bytes=64, name="words_tile"
+            )
+            scales[i] = sbuf.tile(
+                [P, NODES * P], U8, tag="scales", bufs=2, align_bytes=64, name="scales_tile"
+            )
             nc.vector.quantize_mx(
                 out=words[i][:].bitcast(FP8X4),
                 scales=scales[i][:],
@@ -269,20 +262,32 @@ def tile_waveletgatednet_kernel(tc, x, W_words, W_scales, b, threshold, out):
             )
 
 
-        def inverse_level_n1(u):
-            after_n1[u] = unit_tile("after_n1", 2)
+        def level_n1_views(u):
             low, high = slice(0, NODES // 2), slice(NODES // 2, NODES)
-            shared_butterfly(
-                nc, after_n1[u][:, low, :], after_n1[u][:, high, :], kept[u][:, low, :], kept[u][:, high, :]
-            )
+            return after_n1[u][:, low, :], after_n1[u][:, high, :], kept[u][:, low, :], kept[u][:, high, :]
 
-        def inverse_level_n2(u):
+        def difference_n1(u):
+            after_n1[u] = unit_tile("after_n1", 3)
+            out_sum, out_diff, first, second = level_n1_views(u)
+            nc.gpsimd.tensor_tensor(out=out_diff, in0=first, in1=second, op=ALU.subtract)
+
+        def sum_n1(u):
+            out_sum, out_diff, first, second = level_n1_views(u)
+            nc.vector.tensor_tensor(out=out_sum, in0=first, in1=second, op=ALU.add)
+
+        def level_n2_views(u):
             before = after_n1[u][:].rearrange("p (a b c) r -> p a b (c r)", a=2, b=2)
-            after_n2[u] = unit_tile("after_n2", 3)
             after = after_n2[u][:].rearrange("p (a b c) r -> p a b (c r)", a=2, b=2)
-            shared_butterfly(
-                nc, after[:, 0, :, :], after[:, 1, :, :], before[:, :, 0, :], before[:, :, 1, :]
-            )
+            return after[:, 0, :, :], after[:, 1, :, :], before[:, :, 0, :], before[:, :, 1, :]
+
+        def difference_n2(u):
+            after_n2[u] = unit_tile("after_n2", 3)
+            out_sum, out_diff, first, second = level_n2_views(u)
+            nc.gpsimd.tensor_tensor(out=out_diff, in0=first, in1=second, op=ALU.subtract)
+
+        def sum_n2(u):
+            out_sum, out_diff, first, second = level_n2_views(u)
+            nc.vector.tensor_tensor(out=out_sum, in0=first, in1=second, op=ALU.add)
 
         def negate(u):
             negated[u] = unit_tile("negated", 3)
@@ -340,34 +345,39 @@ def tile_waveletgatednet_kernel(tc, x, W_words, W_scales, b, threshold, out):
             return 0 <= u < UNITS
 
         with tc.manual_schedule():
-            for j in range(-2 * E_BLOCKS, UNITS + 2):
-                i, k = divmod(j, E_BLOCKS)
-                if is_unit(j):
-                    gate_coeffs(j)
-                if k == 0 and is_tile(i + 2):
-                    forward_level_1(i + 2)
-                if k == 1 and is_tile(i + 2):
-                    forward_level_2(i + 2)
-                if k == 2 and is_tile(i + 2):
-                    forward_level_3(i + 2)
-                if k == 3 and is_tile(i + 1):
-                    quantise(i + 1)
-                if is_unit(j + 1):
-                    multiply(j + 1)
-                    transpose_coeffs(j + 1)
-                if is_tile((j + 5) // PAIRS):
-                    round_and_transpose((j + 5) // PAIRS, (j + 5) % PAIRS)
-                if k < TENSOR_CHUNKS // BANK_CHUNKS and is_tile(i + 2):
-                    tensor_forward(i + 2, k)
-                if is_unit(j):
-                    keep_large(j)
-                if is_unit(j - 2):
-                    add_residual_and_store(j - 2)
-                if k == 1 and is_tile(i + 3):
-                    load(i + 3)
-                if is_unit(j - 1):
-                    inverse_level_n2(j - 1)
-                    negate(j - 1)
-                    inverse_level_n3(j - 1)
-                if is_unit(j):
-                    inverse_level_n1(j)
+            for s in range(-9, UNITS + 3):
+                if (s + 13) % E_BLOCKS == 0 and is_tile((s + 13) // E_BLOCKS):
+                    load((s + 13) // E_BLOCKS)
+                if is_unit(s):
+                    gate_coeffs(s)
+                if is_unit(s - 3):
+                    add_residual_and_store(s - 3)
+                if is_unit(s - 1):
+                    difference_n1(s - 1)
+                if is_unit(s - 2):
+                    difference_n2(s - 2)
+                    sum_n2(s - 2)
+                i, job = divmod(s + 9, E_BLOCKS)
+                if job == 0 and is_tile(i):
+                    forward_level_1(i)
+                if job == 1 and is_tile(i):
+                    forward_level_2(i)
+                if job == 2 and is_tile(i):
+                    forward_level_3(i)
+                if job == 3 and is_tile(i - 1):
+                    quantise(i - 1)
+                if is_unit(s + 1):
+                    multiply(s + 1)
+                    transpose_coeffs(s + 1)
+                if is_unit(s - 2):
+                    negate(s - 2)
+                if is_tile((s + 6) // PAIRS):
+                    round_and_transpose((s + 6) // PAIRS, (s + 6) % PAIRS)
+                if job < TENSOR_CHUNKS // BANK_CHUNKS and is_tile(i):
+                    tensor_forward(i, job)
+                if is_unit(s - 2):
+                    inverse_level_n3(s - 2)
+                if is_unit(s - 1):
+                    sum_n1(s - 1)
+                if is_unit(s):
+                    keep_large(s)

@@ -116,8 +116,9 @@ def tile_waveletgatednet_kernel(tc, x, W_words, W_scales, b, threshold, out):
         squared = {}
         kept = {}
         after_n1 = {}
-        after_n2 = {}
+        differences = {}
         negated = {}
+        negated_differences = {}
         back = {}
 
         def unit_tile(tag, bufs):
@@ -275,50 +276,61 @@ def tile_waveletgatednet_kernel(tc, x, W_words, W_scales, b, threshold, out):
             out_sum, out_diff, first, second = level_n1_views(u)
             nc.vector.tensor_tensor(out=out_sum, in0=first, in1=second, op=ALU.add)
 
-        def level_n2_views(u):
-            before = after_n1[u][:].rearrange("p (a b c) r -> p a b (c r)", a=2, b=2)
-            after = after_n2[u][:].rearrange("p (a b c) r -> p a b (c r)", a=2, b=2)
-            return after[:, 0, :, :], after[:, 1, :, :], before[:, :, 0, :], before[:, :, 1, :]
-
         def difference_n2(u):
-            after_n2[u] = unit_tile("after_n2", 3)
-            out_sum, out_diff, first, second = level_n2_views(u)
-            nc.gpsimd.tensor_tensor(out=out_diff, in0=first, in1=second, op=ALU.subtract)
+            before = after_n1[u][:].rearrange("p (a b c) r -> p a b (c r)", a=2, b=2)
+            differences[u] = sbuf.tile([P, NODES // 2, P], F32, tag="differences", bufs=3, name="differences_tile")
+            nc.gpsimd.tensor_tensor(
+                out=differences[u][:].rearrange("p (a c) r -> p a (c r)", a=2),
+                in0=before[:, :, 0, :],
+                in1=before[:, :, 1, :],
+                op=ALU.subtract,
+            )
 
-        def sum_n2(u):
-            out_sum, out_diff, first, second = level_n2_views(u)
-            nc.vector.tensor_tensor(out=out_sum, in0=first, in1=second, op=ALU.add)
-
-        def negate(u):
-            negated[u] = unit_tile("negated", 3)
+        def negate_after_n1(u):
+            negated[u] = sbuf.tile([P, NODES // 2, P], F32, tag="negated", bufs=3, name="negated_tile")
             nc.scalar.mul(
-                out=negated[u][:].rearrange("p (m c) r -> p m c r", c=2)[:, :, 1, :],
-                in_=after_n2[u][:].rearrange("p (m c) r -> p m c r", c=2)[:, :, 1, :],
+                out=negated[u][:],
+                in_=after_n1[u][:].rearrange("p (m c) r -> p m c r", c=2)[:, :, 1, :],
                 mul=-1.0,
             )
 
-        def inverse_level_n3(u):
+        def negate_differences(u):
+            negated_differences[u] = sbuf.tile(
+                [P, 2, P], F32, tag="negated_differences", bufs=3, name="negated_differences_tile"
+            )
+            nc.scalar.mul(
+                out=negated_differences[u][:],
+                in_=differences[u][:].rearrange("p (a c) r -> p a c r", c=2)[:, :, 1, :],
+                mul=-1.0,
+            )
+
+        def inverse_levels_n2_n3(u):
             back[u] = []
             for j2 in range(2):
-                second = negated[u] if j2 else after_n2[u]
                 bank = psum.tile([P, 4, P], F32, tag="back", name="back_bank")
                 for m in range(4):
-                    nc.tensor.matmul(
-                        out=bank[:, m, :],
-                        lhsT=after_n2[u][:, 2 * m, :],
-                        rhs=ident_f32[:],
-                        is_transpose=True,
-                        start=True,
-                        stop=False,
-                    )
-                    nc.tensor.matmul(
-                        out=bank[:, m, :],
-                        lhsT=second[:, 2 * m + 1, :],
-                        rhs=ident_f32[:],
-                        is_transpose=True,
-                        start=False,
-                        stop=True,
-                    )
+                    j1, j0 = divmod(m, 2)
+                    if j1 == 0:
+                        terms = [after_n1[u][:, 4 * j0, :], after_n1[u][:, 4 * j0 + 2, :]]
+                        if j2 == 0:
+                            terms += [after_n1[u][:, 4 * j0 + 1, :], after_n1[u][:, 4 * j0 + 3, :]]
+                        else:
+                            terms += [negated[u][:, 2 * j0, :], negated[u][:, 2 * j0 + 1, :]]
+                    else:
+                        terms = [differences[u][:, 2 * j0, :]]
+                        if j2 == 0:
+                            terms += [differences[u][:, 2 * j0 + 1, :]]
+                        else:
+                            terms += [negated_differences[u][:, j0, :]]
+                    for number, term in enumerate(terms):
+                        nc.tensor.matmul(
+                            out=bank[:, m, :],
+                            lhsT=term,
+                            rhs=ident_f32[:],
+                            is_transpose=True,
+                            start=(number == 0),
+                            stop=(number == len(terms) - 1),
+                        )
                 back[u].append(bank)
 
         def add_residual_and_store(u):
@@ -356,7 +368,6 @@ def tile_waveletgatednet_kernel(tc, x, W_words, W_scales, b, threshold, out):
                     difference_n1(s - 1)
                 if is_unit(s - 2):
                     difference_n2(s - 2)
-                    sum_n2(s - 2)
                 i, job = divmod(s + 9, E_BLOCKS)
                 if job == 0 and is_tile(i):
                     forward_level_1(i)
@@ -370,13 +381,14 @@ def tile_waveletgatednet_kernel(tc, x, W_words, W_scales, b, threshold, out):
                     multiply(s + 1)
                     transpose_coeffs(s + 1)
                 if is_unit(s - 2):
-                    negate(s - 2)
+                    negate_after_n1(s - 2)
+                    negate_differences(s - 2)
                 if is_tile((s + 6) // PAIRS):
                     round_and_transpose((s + 6) // PAIRS, (s + 6) % PAIRS)
                 if job < TENSOR_CHUNKS // BANK_CHUNKS and is_tile(i):
                     tensor_forward(i, job)
                 if is_unit(s - 2):
-                    inverse_level_n3(s - 2)
+                    inverse_levels_n2_n3(s - 2)
                 if is_unit(s - 1):
                     sum_n1(s - 1)
                 if is_unit(s):

@@ -107,7 +107,9 @@ def tile_waveletgatednet_kernel(tc, x, W_words, W_scales, b, threshold, out):
         level1 = {}
         level2 = {}
         coeffs = {}
+        rounded = {}
         grouped = {}
+        x_t = {}
         words = {}
         scales = {}
         gates_t = {}
@@ -125,9 +127,7 @@ def tile_waveletgatednet_kernel(tc, x, W_words, W_scales, b, threshold, out):
             return sbuf.tile([P, NODES, P], F32, tag=tag, bufs=bufs, name=tag + "_tile")
 
 
-        def tensor_forward(i, group):
-            if group == 0:
-                coeffs[i] = sbuf.tile([P, NODES, D], F32, tag="coeffs", bufs=3, name="coeffs_tile")
+        def tensor_forward_transpose(i, group):
             first = group * BANK_CHUNKS
             flipped = psum.tile([P, BANK_CHUNKS, P], BF16, tag="flipped")
             for c in range(BANK_CHUNKS):
@@ -136,13 +136,18 @@ def tile_waveletgatednet_kernel(tc, x, W_words, W_scales, b, threshold, out):
                     x_tiles[i][:, (first + c) * P : (first + c + 1) * P],
                     ident_bf16[:],
                 )
-            x_t = sbuf.tile([P, BANK_CHUNKS, P], BF16, tag="x_t", bufs=2)
-            nc.scalar.copy(out=x_t[:], in_=flipped[:])
+            x_t[i, group] = sbuf.tile([P, BANK_CHUNKS, P], BF16, tag="x_t", bufs=2, name="x_t_tile")
+            nc.scalar.copy(out=x_t[i, group][:], in_=flipped[:])
+
+        def tensor_forward_multiply(i, group):
+            if group == 0:
+                coeffs[i] = sbuf.tile([P, NODES, D], F32, tag="coeffs", bufs=3, name="coeffs_tile")
+            first = group * BANK_CHUNKS
             summed = psum.tile([P, BANK_CHUNKS, NODES, CHUNK_D], F32, tag="z_t")
             for c in range(BANK_CHUNKS):
                 nc.tensor.matmul(
                     out=summed[:, c, :, :].rearrange("p n d -> p (n d)"),
-                    lhsT=x_t[:, c, :],
+                    lhsT=x_t[i, group][:, c, :],
                     rhs=haar[:].rearrange("p g b d -> p (g b d)"),
                     start=True,
                     stop=True,
@@ -168,22 +173,34 @@ def tile_waveletgatednet_kernel(tc, x, W_words, W_scales, b, threshold, out):
                 level2[i][:].rearrange("p g b m -> p (g b) m"),
             )
 
-        def round_and_transpose(i, pair):
+        def round_rows(i, pair):
+            if pair == 0:
+                rounded[i] = sbuf.tile([P, NODES, D], BF16, tag="rounded", bufs=2, name="rounded_tile")
+            nodes = slice(2 * pair, 2 * pair + 2)
+            nc.scalar.activation(
+                out=rounded[i][:, nodes, :], in_=coeffs[i][:, nodes, :], func=ACT.Copy, scale=8.0 ** -0.5
+            )
+
+        def transpose_rounded(i, pair):
             if pair == 0:
                 grouped[i] = sbuf.tile(
                     [P, NODES, P, PACK], BF16, tag="grouped", bufs=2, align_bytes=64, name="grouped_tile"
                 )
-            for n in (2 * pair, 2 * pair + 1):
-                by_word = coeffs[i][:, n, :].rearrange("p (q t) -> p t q", t=PACK)
-                flipped = psum.tile([P, PACK, P], F32, tag="flipped")
-                for t in range(PACK):
-                    nc.tensor.transpose(flipped[:, t, :], by_word[:, t, :], ident_f32[:])
-                nc.scalar.activation(
-                    out=grouped[i][:, n, :, :],
-                    in_=flipped[:].rearrange("p t r -> p r t"),
-                    func=ACT.Copy,
-                    scale=8.0 ** -0.5,
-                )
+            flipped = psum.tile([P, 2, 2, P], F32, tag="flipped")
+            for n in range(2):
+                as_words = rounded[i][:, 2 * pair + n, :].bitcast(F32)
+                for h in range(2):
+                    nc.tensor.transpose(flipped[:, n, h, :], as_words[:, h : D // 2 : 2], ident_f32[:])
+            grouped_words = (
+                grouped[i][:]
+                .rearrange("p n r t -> p (n r t)")
+                .bitcast(F32)
+                .rearrange("p (n r h) -> p n r h", n=NODES, h=2)
+            )
+            nc.scalar.copy(
+                out=grouped_words[:, 2 * pair : 2 * pair + 2, :, :],
+                in_=flipped[:].rearrange("p n h r -> p n r h"),
+            )
 
         def quantise(i):
             words[i] = sbuf.tile(
@@ -377,16 +394,22 @@ def tile_waveletgatednet_kernel(tc, x, W_words, W_scales, b, threshold, out):
                     forward_level_3(i)
                 if job == 3 and is_tile(i - 1):
                     quantise(i - 1)
+                plain = job < TENSOR_CHUNKS // BANK_CHUNKS and is_tile(i)
                 if is_unit(s + 1):
                     multiply(s + 1)
+                if plain:
+                    tensor_forward_transpose(i, job)
+                if is_unit(s + 1):
                     transpose_coeffs(s + 1)
                 if is_unit(s - 2):
                     negate_after_n1(s - 2)
                     negate_differences(s - 2)
                 if is_tile((s + 6) // PAIRS):
-                    round_and_transpose((s + 6) // PAIRS, (s + 6) % PAIRS)
-                if job < TENSOR_CHUNKS // BANK_CHUNKS and is_tile(i):
-                    tensor_forward(i, job)
+                    transpose_rounded((s + 6) // PAIRS, (s + 6) % PAIRS)
+                if plain:
+                    tensor_forward_multiply(i, job)
+                if is_tile((s + 7) // PAIRS):
+                    round_rows((s + 7) // PAIRS, (s + 7) % PAIRS)
                 if is_unit(s - 2):
                     inverse_levels_n2_n3(s - 2)
                 if is_unit(s - 1):

@@ -289,13 +289,13 @@ def tile_waveletgatednet_kernel(tc, x, W_words, W_scales, b, threshold, out):
             out_sum, out_diff, first, second = level_n1_views(u)
             nc.gpsimd.tensor_tensor(out=out_diff, in0=first, in1=second, op=ALU.subtract)
 
-        def sum_n1(u):
+        def sum_n1(engine, u):
             out_sum, out_diff, first, second = level_n1_views(u)
-            nc.vector.tensor_tensor(out=out_sum, in0=first, in1=second, op=ALU.add)
+            engine.tensor_tensor(out=out_sum, in0=first, in1=second, op=ALU.add)
 
         def difference_n2(u):
             before = after_n1[u][:].rearrange("p (a b c) r -> p a b (c r)", a=2, b=2)
-            differences[u] = sbuf.tile([P, NODES // 2, P], F32, tag="differences", bufs=3, name="differences_tile")
+            differences[u] = sbuf.tile([P, NODES // 2, P], F32, tag="differences", bufs=2, name="differences_tile")
             nc.gpsimd.tensor_tensor(
                 out=differences[u][:].rearrange("p (a c) r -> p a (c r)", a=2),
                 in0=before[:, :, 0, :],
@@ -303,17 +303,18 @@ def tile_waveletgatednet_kernel(tc, x, W_words, W_scales, b, threshold, out):
                 op=ALU.subtract,
             )
 
-        def negate_after_n1(u):
-            negated[u] = sbuf.tile([P, NODES // 2, P], F32, tag="negated", bufs=3, name="negated_tile")
+
+        def negate_odd_planes(u):
+            negated[u] = sbuf.tile([P, NODES // 2, P], F32, tag="negated", bufs=2, name="negated_tile")
             nc.scalar.mul(
                 out=negated[u][:],
                 in_=after_n1[u][:].rearrange("p (m c) r -> p m c r", c=2)[:, :, 1, :],
                 mul=-1.0,
             )
 
-        def negate_differences(u):
+        def negate_odd_differences(u):
             negated_differences[u] = sbuf.tile(
-                [P, 2, P], F32, tag="negated_differences", bufs=3, name="negated_differences_tile"
+                [P, 2, P], F32, tag="negated_differences", bufs=2, name="negated_differences_tile"
             )
             nc.scalar.mul(
                 out=negated_differences[u][:],
@@ -321,33 +322,48 @@ def tile_waveletgatednet_kernel(tc, x, W_words, W_scales, b, threshold, out):
                 mul=-1.0,
             )
 
+        def negate_three_planes(u, j0):
+            if j0 == 1:
+                negated[u] = sbuf.tile([P, 2, 3, P], F32, tag="negated_three", bufs=2, name="negated_three_tile")
+            nc.scalar.mul(
+                out=negated[u][:, j0, :, :],
+                in_=after_n1[u][:, 4 * j0 + 1 : 4 * j0 + 4, :],
+                mul=-1.0,
+            )
+
+        def terms_of_plane(u, j2, j1, j0):
+            if both_levels_on_tensor(u):
+                return [
+                    negated[u][:, j0, term - 1, :]
+                    if ((term // 2) * j1 + (term % 2) * j2) % 2 == 1
+                    else after_n1[u][:, 4 * j0 + term, :]
+                    for term in range(4)
+                ]
+            if j1 == 0:
+                first = [after_n1[u][:, 4 * j0, :], after_n1[u][:, 4 * j0 + 2, :]]
+                if j2 == 0:
+                    return first + [after_n1[u][:, 4 * j0 + 1, :], after_n1[u][:, 4 * j0 + 3, :]]
+                return first + [negated[u][:, 2 * j0, :], negated[u][:, 2 * j0 + 1, :]]
+            if j2 == 0:
+                return [differences[u][:, 2 * j0, :], differences[u][:, 2 * j0 + 1, :]]
+            return [differences[u][:, 2 * j0, :], negated_differences[u][:, j0, :]]
+
         def inverse_levels_n2_n3(u):
             back[u] = []
             for j2 in range(2):
                 bank = psum.tile([P, 4, P], F32, tag="back", name="back_bank")
-                for m in range(4):
-                    j1, j0 = divmod(m, 2)
-                    if j1 == 0:
-                        terms = [after_n1[u][:, 4 * j0, :], after_n1[u][:, 4 * j0 + 2, :]]
-                        if j2 == 0:
-                            terms += [after_n1[u][:, 4 * j0 + 1, :], after_n1[u][:, 4 * j0 + 3, :]]
-                        else:
-                            terms += [negated[u][:, 2 * j0, :], negated[u][:, 2 * j0 + 1, :]]
-                    else:
-                        terms = [differences[u][:, 2 * j0, :]]
-                        if j2 == 0:
-                            terms += [differences[u][:, 2 * j0 + 1, :]]
-                        else:
-                            terms += [negated_differences[u][:, j0, :]]
-                    for number, term in enumerate(terms):
-                        nc.tensor.matmul(
-                            out=bank[:, m, :],
-                            lhsT=term,
-                            rhs=ident_f32[:],
-                            is_transpose=True,
-                            start=(number == 0),
-                            stop=(number == len(terms) - 1),
-                        )
+                for j0 in (1, 0):
+                    for j1 in range(2):
+                        terms = terms_of_plane(u, j2, j1, j0)
+                        for number, term in enumerate(terms):
+                            nc.tensor.matmul(
+                                out=bank[:, 2 * j1 + j0, :],
+                                lhsT=term,
+                                rhs=ident_f32[:],
+                                is_transpose=True,
+                                start=(number == 0),
+                                stop=(number == len(terms) - 1),
+                            )
                 back[u].append(bank)
 
         def add_residual_and_store(u):
@@ -367,6 +383,9 @@ def tile_waveletgatednet_kernel(tc, x, W_words, W_scales, b, threshold, out):
                 in_=result[:].rearrange("p d h j -> p (d h j)"),
             )
 
+        def both_levels_on_tensor(u):
+            return u % 2 == 0
+
         def is_tile(i):
             return 0 <= i < ROW_TILES
 
@@ -383,7 +402,9 @@ def tile_waveletgatednet_kernel(tc, x, W_words, W_scales, b, threshold, out):
                     add_residual_and_store(s - 3)
                 if is_unit(s - 1):
                     difference_n1(s - 1)
-                if is_unit(s - 2):
+                if is_unit(s - 2) and both_levels_on_tensor(s - 2):
+                    sum_n1(nc.gpsimd, s - 2)
+                if is_unit(s - 2) and not both_levels_on_tensor(s - 2):
                     difference_n2(s - 2)
                 i, job = divmod(s + 9, E_BLOCKS)
                 if job == 0 and is_tile(i):
@@ -401,9 +422,12 @@ def tile_waveletgatednet_kernel(tc, x, W_words, W_scales, b, threshold, out):
                     tensor_forward_transpose(i, job)
                 if is_unit(s + 1):
                     transpose_coeffs(s + 1)
-                if is_unit(s - 2):
-                    negate_after_n1(s - 2)
-                    negate_differences(s - 2)
+                if is_unit(s - 2) and both_levels_on_tensor(s - 2):
+                    negate_three_planes(s - 2, 1)
+                    negate_three_planes(s - 2, 0)
+                if is_unit(s - 2) and not both_levels_on_tensor(s - 2):
+                    negate_odd_planes(s - 2)
+                    negate_odd_differences(s - 2)
                 if is_tile((s + 6) // PAIRS):
                     transpose_rounded((s + 6) // PAIRS, (s + 6) % PAIRS)
                 if plain:
@@ -412,7 +436,7 @@ def tile_waveletgatednet_kernel(tc, x, W_words, W_scales, b, threshold, out):
                     round_rows((s + 7) // PAIRS, (s + 7) % PAIRS)
                 if is_unit(s - 2):
                     inverse_levels_n2_n3(s - 2)
-                if is_unit(s - 1):
-                    sum_n1(s - 1)
+                if is_unit(s - 1) and not both_levels_on_tensor(s - 1):
+                    sum_n1(nc.vector, s - 1)
                 if is_unit(s):
                     keep_large(s)

@@ -31,6 +31,8 @@ TENSOR_L = TENSOR_CHUNKS * P
 TENSOR_D = TENSOR_CHUNKS * CHUNK_D
 VECTOR_L = L - TENSOR_L
 
+LAST_FORWARD_STEP = (ROW_TILES - 1) * E_BLOCKS - 7
+
 FLOPS = 2 * ROWS * NODES * D * D
 
 
@@ -384,7 +386,7 @@ def tile_waveletgatednet_kernel(tc, x, W_words, W_scales, b, threshold, out):
             )
 
         def both_levels_on_tensor(u):
-            return u % 2 == 0
+            return u + 1 <= LAST_FORWARD_STEP
 
         def is_tile(i):
             return 0 <= i < ROW_TILES

@@ -33,6 +33,9 @@ VECTOR_L = L - TENSOR_L
 
 LAST_FORWARD_STEP = (ROW_TILES - 1) * E_BLOCKS - 7
 
+FIRST_MULTIPLY_STEP = -2
+FIRST_TRANSPOSE_STEP = -4
+
 FLOPS = 2 * ROWS * NODES * D * D
 
 
@@ -60,9 +63,11 @@ def tile_waveletgatednet_kernel(tc, x, W_words, W_scales, b, threshold, out):
 
         def load(i):
             x_tiles[i] = sbuf.tile([P, L], BF16, tag="x", bufs=5, name="x_tile")
-            nc.sync.dma_start(out=x_tiles[i][:], in_=x_rows[i * P : (i + 1) * P, :])
+            for part in (slice(TENSOR_L, L), slice(0, TENSOR_L)):
+                nc.sync.dma_start(out=x_tiles[i][:, part], in_=x_rows[i * P : (i + 1) * P, part])
 
         load(0)
+        load(1)
 
         ident_f32 = const.tile([P, P], F32)
         make_identity(nc, ident_f32[:])
@@ -92,19 +97,21 @@ def tile_waveletgatednet_kernel(tc, x, W_words, W_scales, b, threshold, out):
         b_rows = const.tile([P, P], BF16)
         nc.vector.memset(b_rows[:], 0.0)
         nc.sync.dma_start(out=b_rows[0:E_BLOCKS, :], in_=b.rearrange("(k e) -> k e", e=P))
-        b_cols = psum.tile([P, P], BF16, tag="flipped")
-        nc.tensor.transpose(b_cols[:], b_rows[:], ident_bf16[:])
         bias = const.tile([P, E_BLOCKS], F32)
-        nc.vector.tensor_copy(out=bias[:], in_=b_cols[:, 0:E_BLOCKS])
 
         thr_bf16 = const.tile([P, 1], BF16)
         nc.sync.dma_start(out=thr_bf16[:], in_=threshold.partition_broadcast(P))
         thr = const.tile([P, 1], F32)
-        nc.vector.tensor_copy(out=thr[:], in_=thr_bf16[:])
         thr_sq = const.tile([P, 1], F32)
-        nc.vector.scalar_tensor_tensor(
-            out=thr_sq[:], in0=thr[:], scalar=0.125, in1=thr[:], op0=ALU.mult, op1=ALU.mult
-        )
+
+        def finish_constants():
+            b_cols = psum.tile([P, P], BF16, tag="flipped")
+            nc.tensor.transpose(b_cols[:], b_rows[:], ident_bf16[:])
+            nc.vector.tensor_copy(out=bias[:], in_=b_cols[:, 0:E_BLOCKS])
+            nc.vector.tensor_copy(out=thr[:], in_=thr_bf16[:])
+            nc.vector.scalar_tensor_tensor(
+                out=thr_sq[:], in0=thr[:], scalar=0.125, in1=thr[:], op0=ALU.mult, op1=ALU.mult
+            )
 
         level1 = {}
         level2 = {}
@@ -388,6 +395,27 @@ def tile_waveletgatednet_kernel(tc, x, W_words, W_scales, b, threshold, out):
         def both_levels_on_tensor(u):
             return u + 1 <= LAST_FORWARD_STEP
 
+        def plain_groups(s):
+            groups = []
+            i, group = divmod(s + 9, E_BLOCKS)
+            if is_tile(i) and i != 1 and group < TENSOR_CHUNKS // BANK_CHUNKS:
+                groups.append((i, group))
+            if 0 <= s + 8 < TENSOR_CHUNKS // BANK_CHUNKS:
+                groups.append((1, s + 8))
+            return groups
+
+        def pairs_to_round(s):
+            if s == -7:
+                return [(0, pair) for pair in range(PAIRS)]
+            i, pair = divmod(s + 7, PAIRS)
+            return [(i, pair)] if is_tile(i) and i > 0 else []
+
+        def pairs_to_transpose(s):
+            if s in (-6, -5):
+                return [(0, 2 * (s + 6)), (0, 2 * (s + 6) + 1)]
+            i, pair = divmod(s + 6, PAIRS)
+            return [(i, pair)] if is_tile(i) and i > 0 else []
+
         def is_tile(i):
             return 0 <= i < ROW_TILES
 
@@ -396,7 +424,7 @@ def tile_waveletgatednet_kernel(tc, x, W_words, W_scales, b, threshold, out):
 
         with tc.manual_schedule():
             for s in range(-9, UNITS + 3):
-                if (s + 13) % E_BLOCKS == 0 and is_tile((s + 13) // E_BLOCKS):
+                if (s + 13) % E_BLOCKS == 0 and is_tile((s + 13) // E_BLOCKS) and s + 13 >= 2 * E_BLOCKS:
                     load((s + 13) // E_BLOCKS)
                 if is_unit(s):
                     gate_coeffs(s)
@@ -417,25 +445,26 @@ def tile_waveletgatednet_kernel(tc, x, W_words, W_scales, b, threshold, out):
                     forward_level_3(i)
                 if job == 3 and is_tile(i - 1):
                     quantise(i - 1)
-                plain = job < TENSOR_CHUNKS // BANK_CHUNKS and is_tile(i)
-                if is_unit(s + 1):
-                    multiply(s + 1)
-                if plain:
-                    tensor_forward_transpose(i, job)
-                if is_unit(s + 1):
-                    transpose_coeffs(s + 1)
+                if job == 3 and i == 0:
+                    finish_constants()
+                if s == FIRST_MULTIPLY_STEP or s >= 0 and is_unit(s + 1):
+                    multiply(max(s + 1, 0))
+                for tile_and_group in plain_groups(s):
+                    tensor_forward_transpose(*tile_and_group)
+                if s == FIRST_TRANSPOSE_STEP or s >= 0 and is_unit(s + 1):
+                    transpose_coeffs(max(s + 1, 0))
                 if is_unit(s - 2) and both_levels_on_tensor(s - 2):
                     negate_three_planes(s - 2, 1)
                     negate_three_planes(s - 2, 0)
                 if is_unit(s - 2) and not both_levels_on_tensor(s - 2):
                     negate_odd_planes(s - 2)
                     negate_odd_differences(s - 2)
-                if is_tile((s + 6) // PAIRS):
-                    transpose_rounded((s + 6) // PAIRS, (s + 6) % PAIRS)
-                if plain:
-                    tensor_forward_multiply(i, job)
-                if is_tile((s + 7) // PAIRS):
-                    round_rows((s + 7) // PAIRS, (s + 7) % PAIRS)
+                for tile_and_pair in pairs_to_transpose(s):
+                    transpose_rounded(*tile_and_pair)
+                for tile_and_group in plain_groups(s):
+                    tensor_forward_multiply(*tile_and_group)
+                for tile_and_pair in pairs_to_round(s):
+                    round_rows(*tile_and_pair)
                 if is_unit(s - 2):
                     inverse_levels_n2_n3(s - 2)
                 if is_unit(s - 1) and not both_levels_on_tensor(s - 1):

@@ -75,11 +75,13 @@ def tile_waveletgatednet_kernel(tc, x, W_words, W_scales, b, threshold, out):
         make_identity(nc, ident_bf16[:])
 
         haar1 = const.tile([P, 1, 2, P // 2], F32)
-        forward_level(nc, haar1[:], ident_f32[:].unsqueeze(1))
         haar2 = const.tile([P, 2, 2, P // 4], F32)
-        forward_level(nc, haar2[:], haar1[:].rearrange("p g b m -> p (g b) m"))
         haar = const.tile([P, 4, 2, CHUNK_D], BF16)
-        forward_level(nc, haar[:], haar2[:].rearrange("p g b m -> p (g b) m"))
+
+        def make_haar():
+            forward_level(nc, haar1[:], ident_f32[:].unsqueeze(1))
+            forward_level(nc, haar2[:], haar1[:].rearrange("p g b m -> p (g b) m"))
+            forward_level(nc, haar[:], haar2[:].rearrange("p g b m -> p (g b) m"))
 
         w_codes = const.tile([P, D], U32, align_bytes=64)
         nc.sync.dma_start(
@@ -104,10 +106,12 @@ def tile_waveletgatednet_kernel(tc, x, W_words, W_scales, b, threshold, out):
         thr = const.tile([P, 1], F32)
         thr_sq = const.tile([P, 1], F32)
 
-        def finish_constants():
+        def transpose_bias():
             b_cols = psum.tile([P, P], BF16, tag="flipped")
             nc.tensor.transpose(b_cols[:], b_rows[:], ident_bf16[:])
-            nc.vector.tensor_copy(out=bias[:], in_=b_cols[:, 0:E_BLOCKS])
+            nc.scalar.copy(out=bias[:], in_=b_cols[:, 0:E_BLOCKS])
+
+        def finish_threshold():
             nc.vector.tensor_copy(out=thr[:], in_=thr_bf16[:])
             nc.vector.scalar_tensor_tensor(
                 out=thr_sq[:], in0=thr[:], scalar=0.125, in1=thr[:], op0=ALU.mult, op1=ALU.mult
@@ -423,17 +427,23 @@ def tile_waveletgatednet_kernel(tc, x, W_words, W_scales, b, threshold, out):
             return 0 <= u < UNITS
 
         with tc.manual_schedule():
+            make_haar()
             for s in range(-9, UNITS + 3):
                 if (s + 13) % E_BLOCKS == 0 and is_tile((s + 13) // E_BLOCKS) and s + 13 >= 2 * E_BLOCKS:
                     load((s + 13) // E_BLOCKS)
+                if is_unit(s - 2) and both_levels_on_tensor(s - 2):
+                    negate_three_planes(s - 2, 1)
+                    negate_three_planes(s - 2, 0)
+                if is_unit(s - 2) and not both_levels_on_tensor(s - 2):
+                    negate_odd_planes(s - 2)
                 if is_unit(s):
                     gate_coeffs(s)
                 if is_unit(s - 3):
                     add_residual_and_store(s - 3)
                 if is_unit(s - 1):
                     difference_n1(s - 1)
-                if is_unit(s - 2) and both_levels_on_tensor(s - 2):
-                    sum_n1(nc.gpsimd, s - 2)
+                if is_unit(s - 1) and both_levels_on_tensor(s - 1):
+                    sum_n1(nc.gpsimd, s - 1)
                 if is_unit(s - 2) and not both_levels_on_tensor(s - 2):
                     difference_n2(s - 2)
                 i, job = divmod(s + 9, E_BLOCKS)
@@ -446,18 +456,15 @@ def tile_waveletgatednet_kernel(tc, x, W_words, W_scales, b, threshold, out):
                 if job == 3 and is_tile(i - 1):
                     quantise(i - 1)
                 if job == 3 and i == 0:
-                    finish_constants()
+                    transpose_bias()
+                    finish_threshold()
                 if s == FIRST_MULTIPLY_STEP or s >= 0 and is_unit(s + 1):
                     multiply(max(s + 1, 0))
                 for tile_and_group in plain_groups(s):
                     tensor_forward_transpose(*tile_and_group)
                 if s == FIRST_TRANSPOSE_STEP or s >= 0 and is_unit(s + 1):
                     transpose_coeffs(max(s + 1, 0))
-                if is_unit(s - 2) and both_levels_on_tensor(s - 2):
-                    negate_three_planes(s - 2, 1)
-                    negate_three_planes(s - 2, 0)
                 if is_unit(s - 2) and not both_levels_on_tensor(s - 2):
-                    negate_odd_planes(s - 2)
                     negate_odd_differences(s - 2)
                 for tile_and_pair in pairs_to_transpose(s):
                     transpose_rounded(*tile_and_pair)

@@ -25,16 +25,22 @@ UNITS = ROW_TILES * E_BLOCKS
 PAIRS = NODES // 2
 
 CHUNK_D = P // NODES
-TENSOR_CHUNKS = 12
 BANK_CHUNKS = 4
-TENSOR_L = TENSOR_CHUNKS * P
-TENSOR_D = TENSOR_CHUNKS * CHUNK_D
-VECTOR_L = L - TENSOR_L
+
+
+def tensor_groups(i):
+    return 4 if i == 0 else 3
+
+
+def tensor_d(i):
+    return tensor_groups(i) * BANK_CHUNKS * CHUNK_D
+
+
+def tensor_l(i):
+    return tensor_d(i) * NODES
+
 
 LAST_FORWARD_STEP = (ROW_TILES - 1) * E_BLOCKS - 7
-
-FIRST_MULTIPLY_STEP = -2
-FIRST_TRANSPOSE_STEP = -4
 
 FLOPS = 2 * ROWS * NODES * D * D
 
@@ -63,7 +69,7 @@ def tile_waveletgatednet_kernel(tc, x, W_words, W_scales, b, threshold, out):
 
         def load(i):
             x_tiles[i] = sbuf.tile([P, L], BF16, tag="x", bufs=5, name="x_tile")
-            for part in (slice(TENSOR_L, L), slice(0, TENSOR_L)):
+            for part in (slice(tensor_l(i), L), slice(0, tensor_l(i))):
                 nc.sync.dma_start(out=x_tiles[i][:, part], in_=x_rows[i * P : (i + 1) * P, part])
 
         load(0)
@@ -117,6 +123,10 @@ def tile_waveletgatednet_kernel(tc, x, W_words, W_scales, b, threshold, out):
                 out=thr_sq[:], in0=thr[:], scalar=0.125, in1=thr[:], op0=ALU.mult, op1=ALU.mult
             )
 
+        def load_sigmoid_table():
+            nc.vector.memset(thr_sq[:], 0.0)
+            nc.scalar.activation(out=thr_sq[:], in_=thr_sq[:], func=ACT.Sigmoid)
+
         level1 = {}
         level2 = {}
         coeffs = {}
@@ -131,9 +141,11 @@ def tile_waveletgatednet_kernel(tc, x, W_words, W_scales, b, threshold, out):
         squared = {}
         kept = {}
         after_n1 = {}
-        differences = {}
         negated = {}
-        negated_differences = {}
+        flipped_chunks = {}
+        summed_chunks = {}
+        flipped_pairs = {}
+        z_t = {}
         back = {}
 
         def unit_tile(tag, bufs):
@@ -149,12 +161,18 @@ def tile_waveletgatednet_kernel(tc, x, W_words, W_scales, b, threshold, out):
                     x_tiles[i][:, (first + c) * P : (first + c + 1) * P],
                     ident_bf16[:],
                 )
+            flipped_chunks[i, group] = flipped
+
+        def keep_flipped_chunks(i, group):
             x_t[i, group] = sbuf.tile([P, BANK_CHUNKS, P], BF16, tag="x_t", bufs=2, name="x_t_tile")
-            nc.scalar.copy(out=x_t[i, group][:], in_=flipped[:])
+            nc.scalar.copy(out=x_t[i, group][:], in_=flipped_chunks[i, group][:])
+
+        def new_coeffs(i):
+            if i not in coeffs:
+                coeffs[i] = sbuf.tile([P, NODES, D], F32, tag="coeffs", bufs=3, name="coeffs_tile")
 
         def tensor_forward_multiply(i, group):
-            if group == 0:
-                coeffs[i] = sbuf.tile([P, NODES, D], F32, tag="coeffs", bufs=3, name="coeffs_tile")
+            new_coeffs(i)
             first = group * BANK_CHUNKS
             summed = psum.tile([P, BANK_CHUNKS, NODES, CHUNK_D], F32, tag="z_t")
             for c in range(BANK_CHUNKS):
@@ -165,45 +183,64 @@ def tile_waveletgatednet_kernel(tc, x, W_words, W_scales, b, threshold, out):
                     start=True,
                     stop=True,
                 )
+            summed_chunks[i, group] = summed
+
+        def keep_summed_chunks(i, group):
+            first = group * BANK_CHUNKS
             d_range = slice(first * CHUNK_D, (first + BANK_CHUNKS) * CHUNK_D)
             nc.scalar.copy(
                 out=coeffs[i][:, :, d_range].rearrange("p n (c d) -> p n c d", c=BANK_CHUNKS),
-                in_=summed[:].rearrange("p c n d -> p n c d"),
+                in_=summed_chunks[i, group][:].rearrange("p c n d -> p n c d"),
             )
 
         def forward_level_1(i):
-            level1[i] = sbuf.tile([P, 1, 2, VECTOR_L // 2], F32, tag="level1", name="level1_tile")
-            forward_level(nc, level1[i][:], x_tiles[i][:, TENSOR_L:L].unsqueeze(1))
+            samples = L - tensor_l(i)
+            level1[i] = sbuf.tile([P, 1, 2, samples // 2], F32, tag="level1", name="level1_tile")
+            forward_level(nc, level1[i][:], x_tiles[i][:, tensor_l(i) : L].unsqueeze(1))
 
         def forward_level_2(i):
-            level2[i] = sbuf.tile([P, 2, 2, VECTOR_L // 4], F32, tag="level2", name="level2_tile")
+            samples = L - tensor_l(i)
+            level2[i] = sbuf.tile([P, 2, 2, samples // 4], F32, tag="level2", name="level2_tile")
             forward_level(nc, level2[i][:], level1[i][:].rearrange("p g b m -> p (g b) m"))
 
         def forward_level_3(i):
+            new_coeffs(i)
             forward_level(
                 nc,
-                coeffs[i][:, :, TENSOR_D:D].rearrange("p (g b) d -> p g b d", b=2),
+                coeffs[i][:, :, tensor_d(i) : D].rearrange("p (g b) d -> p g b d", b=2),
                 level2[i][:].rearrange("p g b m -> p (g b) m"),
             )
 
-        def round_rows(i, pair):
-            if pair == 0:
+        def round_rows(i, pair, on_vector=False):
+            if i not in rounded:
                 rounded[i] = sbuf.tile([P, NODES, D], BF16, tag="rounded", bufs=2, name="rounded_tile")
             nodes = slice(2 * pair, 2 * pair + 2)
-            nc.scalar.activation(
-                out=rounded[i][:, nodes, :], in_=coeffs[i][:, nodes, :], func=ACT.Copy, scale=8.0 ** -0.5
-            )
+            if on_vector:
+                nc.vector.tensor_scalar(
+                    out=rounded[i][:, nodes, :],
+                    in0=coeffs[i][:, nodes, :],
+                    scalar1=8.0 ** -0.5,
+                    scalar2=None,
+                    op0=ALU.mult,
+                )
+            else:
+                nc.scalar.activation(
+                    out=rounded[i][:, nodes, :], in_=coeffs[i][:, nodes, :], func=ACT.Copy, scale=8.0 ** -0.5
+                )
 
         def transpose_rounded(i, pair):
-            if pair == 0:
-                grouped[i] = sbuf.tile(
-                    [P, NODES, P, PACK], BF16, tag="grouped", bufs=2, align_bytes=64, name="grouped_tile"
-                )
             flipped = psum.tile([P, 2, 2, P], F32, tag="flipped")
             for n in range(2):
                 as_words = rounded[i][:, 2 * pair + n, :].bitcast(F32)
                 for h in range(2):
                     nc.tensor.transpose(flipped[:, n, h, :], as_words[:, h : D // 2 : 2], ident_f32[:])
+            flipped_pairs[i, pair] = flipped
+
+        def keep_flipped_pair(i, pair):
+            if i not in grouped:
+                grouped[i] = sbuf.tile(
+                    [P, NODES, P, PACK], BF16, tag="grouped", bufs=2, align_bytes=64, name="grouped_tile"
+                )
             grouped_words = (
                 grouped[i][:]
                 .rearrange("p n r t -> p (n r t)")
@@ -212,7 +249,7 @@ def tile_waveletgatednet_kernel(tc, x, W_words, W_scales, b, threshold, out):
             )
             nc.scalar.copy(
                 out=grouped_words[:, 2 * pair : 2 * pair + 2, :, :],
-                in_=flipped[:].rearrange("p n h r -> p n r h"),
+                in_=flipped_pairs[i, pair][:].rearrange("p n h r -> p n r h"),
             )
 
         def quantise(i):
@@ -232,12 +269,12 @@ def tile_waveletgatednet_kernel(tc, x, W_words, W_scales, b, threshold, out):
         def multiply(u):
             i, k = divmod(u, E_BLOCKS)
             e_cols = slice(k * P, (k + 1) * P)
-            gates_t[u] = unit_tile("gates_t", 2)
+            z_t[u] = []
             for c in range(NODES * P // N_MOVING):
                 cols = slice(c * N_MOVING, (c + 1) * N_MOVING)
-                z_t = psum.tile([P, N_MOVING], F32, tag="z_t")
+                bank = psum.tile([P, N_MOVING], F32, tag="z_t", name="z_t_bank")
                 nc.tensor.matmul_mx(
-                    out=z_t[:],
+                    out=bank[:],
                     lhsT=w_codes[:, e_cols].bitcast(FP8X4),
                     lhsT_scale=w_scales[:, e_cols],
                     rhs=words[i][:, cols].bitcast(FP8X4),
@@ -245,13 +282,19 @@ def tile_waveletgatednet_kernel(tc, x, W_words, W_scales, b, threshold, out):
                     start=True,
                     stop=True,
                 )
-                nc.scalar.activation(
-                    out=gates_t[u][:].rearrange("p n r -> p (n r)")[:, cols],
-                    in_=z_t[:],
-                    func=ACT.Sigmoid,
-                    bias=bias[:, k : k + 1],
-                    scale=1.0,
-                )
+                z_t[u].append(bank)
+
+        def sigmoid(u, c):
+            k = u % E_BLOCKS
+            if c == 0:
+                gates_t[u] = unit_tile("gates_t", 2)
+            nc.scalar.activation(
+                out=gates_t[u][:].rearrange("p n r -> p (n r)")[:, c * N_MOVING : (c + 1) * N_MOVING],
+                in_=z_t[u][c][:],
+                func=ACT.Sigmoid,
+                bias=bias[:, k : k + 1],
+                scale=1.0,
+            )
 
         def transpose_coeffs(u):
             i, k = divmod(u, E_BLOCKS)
@@ -278,6 +321,8 @@ def tile_waveletgatednet_kernel(tc, x, W_words, W_scales, b, threshold, out):
                     op0=ALU.mult,
                     op1=ALU.mult,
                 )
+
+        def square(u):
             squared[u] = unit_tile("squared", 2)
             nc.scalar.activation(out=squared[u][:], in_=product[u][:], func=ACT.Square)
 
@@ -293,91 +338,70 @@ def tile_waveletgatednet_kernel(tc, x, W_words, W_scales, b, threshold, out):
             )
 
 
-        def level_n1_views(u):
-            low, high = slice(0, NODES // 2), slice(NODES // 2, NODES)
-            return after_n1[u][:, low, :], after_n1[u][:, high, :], kept[u][:, low, :], kept[u][:, high, :]
+        def half_n1(u, j0):
+            first = 4 * (1 - j0)
+            return after_n1[u][:, first : first + NODES // 2, :]
 
         def difference_n1(u):
-            after_n1[u] = unit_tile("after_n1", 3)
-            out_sum, out_diff, first, second = level_n1_views(u)
-            nc.gpsimd.tensor_tensor(out=out_diff, in0=first, in1=second, op=ALU.subtract)
+            planes = NODES if both_levels_on_tensor(u) else NODES + 4
+            after_n1[u] = sbuf.tile([P, planes, P], F32, tag="after_n1", bufs=3, name="after_n1_tile")
+            nc.gpsimd.tensor_tensor(
+                out=half_n1(u, 1), in0=kept[u][:, 0:4, :], in1=kept[u][:, 4:8, :], op=ALU.subtract
+            )
 
         def sum_n1(engine, u):
-            out_sum, out_diff, first, second = level_n1_views(u)
-            engine.tensor_tensor(out=out_sum, in0=first, in1=second, op=ALU.add)
+            engine.tensor_tensor(out=half_n1(u, 0), in0=kept[u][:, 0:4, :], in1=kept[u][:, 4:8, :], op=ALU.add)
 
-        def difference_n2(u):
-            before = after_n1[u][:].rearrange("p (a b c) r -> p a b (c r)", a=2, b=2)
-            differences[u] = sbuf.tile([P, NODES // 2, P], F32, tag="differences", bufs=2, name="differences_tile")
-            nc.gpsimd.tensor_tensor(
-                out=differences[u][:].rearrange("p (a c) r -> p a (c r)", a=2),
-                in0=before[:, :, 0, :],
-                in1=before[:, :, 1, :],
-                op=ALU.subtract,
+        def level_n2_of_half(engine, u, j1):
+            engine.tensor_tensor(
+                out=after_n1[u][:, NODES + 2 * j1 : NODES + 2 * j1 + 2, :],
+                in0=half_n1(u, 1)[:, 0:2, :],
+                in1=half_n1(u, 1)[:, 2:4, :],
+                op=ALU.add if j1 == 0 else ALU.subtract,
             )
 
 
-        def negate_odd_planes(u):
-            negated[u] = sbuf.tile([P, NODES // 2, P], F32, tag="negated", bufs=2, name="negated_tile")
-            nc.scalar.mul(
-                out=negated[u][:],
-                in_=after_n1[u][:].rearrange("p (m c) r -> p m c r", c=2)[:, :, 1, :],
-                mul=-1.0,
-            )
-
-        def negate_odd_differences(u):
-            negated_differences[u] = sbuf.tile(
-                [P, 2, P], F32, tag="negated_differences", bufs=2, name="negated_differences_tile"
-            )
-            nc.scalar.mul(
-                out=negated_differences[u][:],
-                in_=differences[u][:].rearrange("p (a c) r -> p a c r", c=2)[:, :, 1, :],
-                mul=-1.0,
-            )
-
-        def negate_three_planes(u, j0):
+        def negate(u, j0):
             if j0 == 1:
-                negated[u] = sbuf.tile([P, 2, 3, P], F32, tag="negated_three", bufs=2, name="negated_three_tile")
-            nc.scalar.mul(
-                out=negated[u][:, j0, :, :],
-                in_=after_n1[u][:, 4 * j0 + 1 : 4 * j0 + 4, :],
-                mul=-1.0,
-            )
+                negated[u] = sbuf.tile([P, 2, 3, P], F32, tag="negated", bufs=2, name="negated_tile")
+            if j0 == 0 or both_levels_on_tensor(u):
+                nc.scalar.mul(out=negated[u][:, j0, :, :], in_=half_n1(u, j0)[:, 1:4, :], mul=-1.0)
+            else:
+                nc.scalar.mul(
+                    out=negated[u][:, j0, 0:2, :],
+                    in_=after_n1[u][:, NODES : NODES + 4, :].rearrange("p (j c) r -> p j c r", c=2)[:, :, 1, :],
+                    mul=-1.0,
+                )
 
         def terms_of_plane(u, j2, j1, j0):
-            if both_levels_on_tensor(u):
+            if j0 == 0 or both_levels_on_tensor(u):
                 return [
                     negated[u][:, j0, term - 1, :]
                     if ((term // 2) * j1 + (term % 2) * j2) % 2 == 1
-                    else after_n1[u][:, 4 * j0 + term, :]
+                    else half_n1(u, j0)[:, term, :]
                     for term in range(4)
                 ]
-            if j1 == 0:
-                first = [after_n1[u][:, 4 * j0, :], after_n1[u][:, 4 * j0 + 2, :]]
-                if j2 == 0:
-                    return first + [after_n1[u][:, 4 * j0 + 1, :], after_n1[u][:, 4 * j0 + 3, :]]
-                return first + [negated[u][:, 2 * j0, :], negated[u][:, 2 * j0 + 1, :]]
-            if j2 == 0:
-                return [differences[u][:, 2 * j0, :], differences[u][:, 2 * j0 + 1, :]]
-            return [differences[u][:, 2 * j0, :], negated_differences[u][:, j0, :]]
+            first = NODES + 2 * j1
+            return [
+                after_n1[u][:, first, :],
+                negated[u][:, j0, j1, :] if j2 == 1 else after_n1[u][:, first + 1, :],
+            ]
 
-        def inverse_levels_n2_n3(u):
-            back[u] = []
-            for j2 in range(2):
-                bank = psum.tile([P, 4, P], F32, tag="back", name="back_bank")
-                for j0 in (1, 0):
-                    for j1 in range(2):
-                        terms = terms_of_plane(u, j2, j1, j0)
-                        for number, term in enumerate(terms):
-                            nc.tensor.matmul(
-                                out=bank[:, 2 * j1 + j0, :],
-                                lhsT=term,
-                                rhs=ident_f32[:],
-                                is_transpose=True,
-                                start=(number == 0),
-                                stop=(number == len(terms) - 1),
-                            )
-                back[u].append(bank)
+        def inverse_levels_n2_n3(u, j2):
+            bank = psum.tile([P, 4, P], F32, tag="back", name="back_bank")
+            for j0 in (1, 0):
+                for j1 in range(2):
+                    terms = terms_of_plane(u, j2, j1, j0)
+                    for number, term in enumerate(terms):
+                        nc.tensor.matmul(
+                            out=bank[:, 2 * j1 + j0, :],
+                            lhsT=term,
+                            rhs=ident_f32[:],
+                            is_transpose=True,
+                            start=(number == 0),
+                            stop=(number == len(terms) - 1),
+                        )
+            back[u, j2] = bank
 
         def add_residual_and_store(u):
             i, k = divmod(u, E_BLOCKS)
@@ -387,7 +411,7 @@ def tile_waveletgatednet_kernel(tc, x, W_words, W_scales, b, threshold, out):
             for j2 in range(2):
                 nc.vector.tensor_tensor(
                     out=result[:, :, j2, :],
-                    in0=back[u][j2][:].rearrange("p j d -> p d j"),
+                    in0=back[u, j2][:].rearrange("p j d -> p d j"),
                     in1=samples[:, :, j2, :],
                     op=ALU.add,
                 )
@@ -399,26 +423,30 @@ def tile_waveletgatednet_kernel(tc, x, W_words, W_scales, b, threshold, out):
         def both_levels_on_tensor(u):
             return u + 1 <= LAST_FORWARD_STEP
 
-        def plain_groups(s):
-            groups = []
+        def forward_jobs(s):
+            early = {0: [(1, forward_level_3)], 1: [(2, forward_level_1), (2, forward_level_2)], 2: [(2, forward_level_3)]}
+            if s in early:
+                return early[s]
+            i, job = divmod(s + 9, E_BLOCKS)
+            return [(i, (forward_level_1, forward_level_2, forward_level_3)[job])] if is_tile(i) and job < 3 else []
+
+        def groups_to_transform(s):
+            if s in (0, 1, 2):
+                return [(2, s)]
             i, group = divmod(s + 9, E_BLOCKS)
-            if is_tile(i) and i != 1 and group < TENSOR_CHUNKS // BANK_CHUNKS:
-                groups.append((i, group))
-            if 0 <= s + 8 < TENSOR_CHUNKS // BANK_CHUNKS:
-                groups.append((1, s + 8))
-            return groups
+            return [(i, group)] if is_tile(i) and group < tensor_groups(i) else []
 
         def pairs_to_round(s):
-            if s == -7:
-                return [(0, pair) for pair in range(PAIRS)]
+            early = {0: [(1, 0), (1, 2)], 1: [], 2: [(2, 0)], 3: [(2, 1), (2, 2)], 4: [(2, 3)]}
+            if s in early:
+                return early[s]
             i, pair = divmod(s + 7, PAIRS)
-            return [(i, pair)] if is_tile(i) and i > 0 else []
+            return [(i, pair)] if is_tile(i) else []
 
         def pairs_to_transpose(s):
-            if s in (-6, -5):
-                return [(0, 2 * (s + 6)), (0, 2 * (s + 6) + 1)]
-            i, pair = divmod(s + 6, PAIRS)
-            return [(i, pair)] if is_tile(i) and i > 0 else []
+            if s == 1:
+                return [(1, 1), (1, 0), (1, 3), (1, 2)]
+            return pairs_to_round(s - 1) if s > 0 else []
 
         def is_tile(i):
             return 0 <= i < ROW_TILES
@@ -428,53 +456,97 @@ def tile_waveletgatednet_kernel(tc, x, W_words, W_scales, b, threshold, out):
 
         with tc.manual_schedule():
             make_haar()
-            for s in range(-9, UNITS + 3):
-                if (s + 13) % E_BLOCKS == 0 and is_tile((s + 13) // E_BLOCKS) and s + 13 >= 2 * E_BLOCKS:
+            load_sigmoid_table()
+            load(2)
+            load(3)
+            for level in (forward_level_1, forward_level_2, forward_level_3):
+                level(0)
+            groups = [(0, group) for group in range(tensor_groups(0))] + [(1, 0)]
+            for number, group in enumerate(groups):
+                tensor_forward_transpose(*group)
+                keep_flipped_chunks(*group)
+                if number > 0:
+                    tensor_forward_multiply(*groups[number - 1])
+                    keep_summed_chunks(*groups[number - 1])
+            tensor_forward_multiply(1, 0)
+            transpose_coeffs(0)
+            round_rows(0, 1, on_vector=True)
+            round_rows(0, 3, on_vector=True)
+            round_rows(0, 0)
+            transpose_rounded(0, 1)
+            keep_flipped_pair(0, 1)
+            round_rows(0, 2)
+            for pair in (3, 0, 2):
+                transpose_rounded(0, pair)
+                keep_flipped_pair(0, pair)
+            keep_summed_chunks(1, 0)
+            forward_level_1(1)
+            finish_threshold()
+            quantise(0)
+            for group in (1, 2):
+                tensor_forward_transpose(1, group)
+                keep_flipped_chunks(1, group)
+            transpose_bias()
+            multiply(0)
+            sigmoid(0, 0)
+            sigmoid(0, 1)
+            for group in (1, 2):
+                tensor_forward_multiply(1, group)
+                keep_summed_chunks(1, group)
+            forward_level_2(1)
+            for s in range(UNITS + 3):
+                if (s + 13) % E_BLOCKS == 0 and is_tile((s + 13) // E_BLOCKS):
                     load((s + 13) // E_BLOCKS)
-                if is_unit(s - 2) and both_levels_on_tensor(s - 2):
-                    negate_three_planes(s - 2, 1)
-                    negate_three_planes(s - 2, 0)
-                if is_unit(s - 2) and not both_levels_on_tensor(s - 2):
-                    negate_odd_planes(s - 2)
+                if is_unit(s - 2):
+                    negate(s - 2, 1)
                 if is_unit(s):
                     gate_coeffs(s)
+                    square(s)
                 if is_unit(s - 3):
                     add_residual_and_store(s - 3)
                 if is_unit(s - 1):
                     difference_n1(s - 1)
                 if is_unit(s - 1) and both_levels_on_tensor(s - 1):
                     sum_n1(nc.gpsimd, s - 1)
-                if is_unit(s - 2) and not both_levels_on_tensor(s - 2):
-                    difference_n2(s - 2)
-                i, job = divmod(s + 9, E_BLOCKS)
-                if job == 0 and is_tile(i):
-                    forward_level_1(i)
-                if job == 1 and is_tile(i):
-                    forward_level_2(i)
-                if job == 2 and is_tile(i):
-                    forward_level_3(i)
-                if job == 3 and is_tile(i - 1):
-                    quantise(i - 1)
-                if job == 3 and i == 0:
-                    transpose_bias()
-                    finish_threshold()
-                if s == FIRST_MULTIPLY_STEP or s >= 0 and is_unit(s + 1):
-                    multiply(max(s + 1, 0))
-                for tile_and_group in plain_groups(s):
+                if is_unit(s - 1) and not both_levels_on_tensor(s - 1):
+                    level_n2_of_half(nc.gpsimd, s - 1, 1)
+                if (s + 2) % E_BLOCKS == 0 and is_tile((s + 2) // E_BLOCKS):
+                    quantise((s + 2) // E_BLOCKS)
+                for i, level in forward_jobs(s):
+                    level(i)
+                if s == 0:
+                    round_rows(1, 1, on_vector=True)
+                    round_rows(1, 3, on_vector=True)
+                if is_unit(s + 1):
+                    multiply(s + 1)
+                    sigmoid(s + 1, 0)
+                for tile_and_group in groups_to_transform(s):
                     tensor_forward_transpose(*tile_and_group)
-                if s == FIRST_TRANSPOSE_STEP or s >= 0 and is_unit(s + 1):
-                    transpose_coeffs(max(s + 1, 0))
-                if is_unit(s - 2) and not both_levels_on_tensor(s - 2):
-                    negate_odd_differences(s - 2)
-                for tile_and_pair in pairs_to_transpose(s):
+                    keep_flipped_chunks(*tile_and_group)
+                if is_unit(s - 2):
+                    negate(s - 2, 0)
+                if is_unit(s + 1):
+                    transpose_coeffs(s + 1)
+                for tile_and_pair in pairs_to_transpose(s)[:1]:
                     transpose_rounded(*tile_and_pair)
-                for tile_and_group in plain_groups(s):
+                for tile_and_group in groups_to_transform(s):
                     tensor_forward_multiply(*tile_and_group)
+                if is_unit(s + 1):
+                    sigmoid(s + 1, 1)
+                for tile_and_group in groups_to_transform(s):
+                    keep_summed_chunks(*tile_and_group)
                 for tile_and_pair in pairs_to_round(s):
                     round_rows(*tile_and_pair)
                 if is_unit(s - 2):
-                    inverse_levels_n2_n3(s - 2)
+                    inverse_levels_n2_n3(s - 2, 0)
+                for number, tile_and_pair in enumerate(pairs_to_transpose(s)):
+                    if number > 0:
+                        transpose_rounded(*tile_and_pair)
+                    keep_flipped_pair(*tile_and_pair)
+                if is_unit(s - 2):
+                    inverse_levels_n2_n3(s - 2, 1)
                 if is_unit(s - 1) and not both_levels_on_tensor(s - 1):
                     sum_n1(nc.vector, s - 1)
+                    level_n2_of_half(nc.vector, s - 1, 0)
                 if is_unit(s):
                     keep_large(s)

@@ -349,8 +349,9 @@ def tile_waveletgatednet_kernel(tc, x, W_words, W_scales, b, threshold, out):
                 out=half_n1(u, 1), in0=kept[u][:, 0:4, :], in1=kept[u][:, 4:8, :], op=ALU.subtract
             )
 
-        def sum_n1(engine, u):
-            engine.tensor_tensor(out=half_n1(u, 0), in0=kept[u][:, 0:4, :], in1=kept[u][:, 4:8, :], op=ALU.add)
+        def sum_n1(engine, u, planes=slice(0, NODES // 2)):
+            low, high = (kept[u][:, first : first + NODES // 2, :][:, planes, :] for first in (0, NODES // 2))
+            engine.tensor_tensor(out=half_n1(u, 0)[:, planes, :], in0=low, in1=high, op=ALU.add)
 
         def level_n2_of_half(engine, u, j1):
             engine.tensor_tensor(
@@ -507,7 +508,7 @@ def tile_waveletgatednet_kernel(tc, x, W_words, W_scales, b, threshold, out):
                 if is_unit(s - 1):
                     difference_n1(s - 1)
                 if is_unit(s - 1) and both_levels_on_tensor(s - 1):
-                    sum_n1(nc.gpsimd, s - 1)
+                    sum_n1(nc.gpsimd, s - 1, slice(2, 4))
                 if is_unit(s - 1) and not both_levels_on_tensor(s - 1):
                     level_n2_of_half(nc.gpsimd, s - 1, 1)
                 if (s + 2) % E_BLOCKS == 0 and is_tile((s + 2) // E_BLOCKS):
@@ -545,6 +546,8 @@ def tile_waveletgatednet_kernel(tc, x, W_words, W_scales, b, threshold, out):
                     keep_flipped_pair(*tile_and_pair)
                 if is_unit(s - 2):
                     inverse_levels_n2_n3(s - 2, 1)
+                if is_unit(s - 1) and both_levels_on_tensor(s - 1):
+                    sum_n1(nc.vector, s - 1, slice(0, 2))
                 if is_unit(s - 1) and not both_levels_on_tensor(s - 1):
                     sum_n1(nc.vector, s - 1)
                     level_n2_of_half(nc.vector, s - 1, 0)

@@ -42,17 +42,23 @@ def tensor_l(i):
 
 LAST_FORWARD_STEP = (ROW_TILES - 1) * E_BLOCKS - 7
 
+FIRST_PIECES = 2
+
 FLOPS = 2 * ROWS * NODES * D * D
 
 
-def butterfly(nc, out_sum, out_diff, first, second):
-    nc.vector.tensor_tensor(out=out_sum, in0=first, in1=second, op=ALU.add)
-    nc.vector.tensor_tensor(out=out_diff, in0=first, in1=second, op=ALU.subtract)
+SUM, DIFFERENCE = 0, 1
 
 
-def forward_level(nc, out, in_):
+def forward_level(nc, out, in_, halves=(SUM, DIFFERENCE)):
     pairs = in_.rearrange("p g (m two) -> p g two m", two=2)
-    butterfly(nc, out[:, :, 0, :], out[:, :, 1, :], pairs[:, :, 0, :], pairs[:, :, 1, :])
+    for half in halves:
+        nc.vector.tensor_tensor(
+            out=out[:, :, half, :],
+            in0=pairs[:, :, 0, :],
+            in1=pairs[:, :, 1, :],
+            op=ALU.add if half == SUM else ALU.subtract,
+        )
 
 
 def tile_waveletgatednet_kernel(tc, x, W_words, W_scales, b, threshold, out):
@@ -69,7 +75,10 @@ def tile_waveletgatednet_kernel(tc, x, W_words, W_scales, b, threshold, out):
 
         def load(i):
             x_tiles[i] = sbuf.tile([P, L], BF16, tag="x", bufs=5, name="x_tile")
-            for part in (slice(tensor_l(i), L), slice(0, tensor_l(i))):
+            pieces = FIRST_PIECES if i == 0 else 1
+            samples = (L - tensor_l(i)) // pieces
+            parts = [slice(first, first + samples) for first in range(tensor_l(i), L, samples)]
+            for part in parts + [slice(0, tensor_l(i))]:
                 nc.sync.dma_start(out=x_tiles[i][:, part], in_=x_rows[i * P : (i + 1) * P, part])
 
         load(0)
@@ -194,14 +203,21 @@ def tile_waveletgatednet_kernel(tc, x, W_words, W_scales, b, threshold, out):
             )
 
         def forward_level_1(i):
-            samples = L - tensor_l(i)
-            level1[i] = sbuf.tile([P, 1, 2, samples // 2], F32, tag="level1", name="level1_tile")
-            forward_level(nc, level1[i][:], x_tiles[i][:, tensor_l(i) : L].unsqueeze(1))
+            pieces = FIRST_PIECES if i == 0 else 1
+            outputs = (L - tensor_l(i)) // 2
+            level1[i] = sbuf.tile([P, 1, 2, outputs], F32, tag="level1", name="level1_tile")
+            step = outputs // pieces
+            for m in range(0, outputs, step):
+                first = tensor_l(i) + 2 * m
+                forward_level(
+                    nc, level1[i][:, :, :, m : m + step], x_tiles[i][:, first : first + 2 * step].unsqueeze(1)
+                )
 
-        def forward_level_2(i):
-            samples = L - tensor_l(i)
-            level2[i] = sbuf.tile([P, 2, 2, samples // 4], F32, tag="level2", name="level2_tile")
-            forward_level(nc, level2[i][:], level1[i][:].rearrange("p g b m -> p (g b) m"))
+        def forward_level_2(i, halves=(SUM, DIFFERENCE)):
+            if i not in level2:
+                outputs = (L - tensor_l(i)) // 4
+                level2[i] = sbuf.tile([P, 2, 2, outputs], F32, tag="level2", name="level2_tile")
+            forward_level(nc, level2[i][:], level1[i][:].rearrange("p g b m -> p (g b) m"), halves)
 
         def forward_level_3(i):
             new_coeffs(i)
@@ -342,10 +358,10 @@ def tile_waveletgatednet_kernel(tc, x, W_words, W_scales, b, threshold, out):
             first = 4 * (1 - j0)
             return after_n1[u][:, first : first + NODES // 2, :]
 
-        def difference_n1(u):
+        def difference_n1(engine, u):
             planes = NODES if both_levels_on_tensor(u) else NODES + 4
             after_n1[u] = sbuf.tile([P, planes, P], F32, tag="after_n1", bufs=3, name="after_n1_tile")
-            nc.gpsimd.tensor_tensor(
+            engine.tensor_tensor(
                 out=half_n1(u, 1), in0=kept[u][:, 0:4, :], in1=kept[u][:, 4:8, :], op=ALU.subtract
             )
 
@@ -438,7 +454,7 @@ def tile_waveletgatednet_kernel(tc, x, W_words, W_scales, b, threshold, out):
             return [(i, group)] if is_tile(i) and group < tensor_groups(i) else []
 
         def pairs_to_round(s):
-            early = {0: [(1, 0), (1, 2)], 1: [], 2: [(2, 0)], 3: [(2, 1), (2, 2)], 4: [(2, 3)]}
+            early = {0: [(1, 0), (1, 1), (1, 2)], 1: [], 2: [(2, 0)], 3: [(2, 1), (2, 2)], 4: [(2, 3)]}
             if s in early:
                 return early[s]
             i, pair = divmod(s + 7, PAIRS)
@@ -446,7 +462,7 @@ def tile_waveletgatednet_kernel(tc, x, W_words, W_scales, b, threshold, out):
 
         def pairs_to_transpose(s):
             if s == 1:
-                return [(1, 1), (1, 0), (1, 3), (1, 2)]
+                return [(1, 0), (1, 1), (1, 3), (1, 2)]
             return pairs_to_round(s - 1) if s > 0 else []
 
         def is_tile(i):
@@ -483,6 +499,7 @@ def tile_waveletgatednet_kernel(tc, x, W_words, W_scales, b, threshold, out):
             keep_summed_chunks(1, 0)
             forward_level_1(1)
             finish_threshold()
+            forward_level_2(1, [SUM])
             quantise(0)
             for group in (1, 2):
                 tensor_forward_transpose(1, group)
@@ -494,7 +511,7 @@ def tile_waveletgatednet_kernel(tc, x, W_words, W_scales, b, threshold, out):
             for group in (1, 2):
                 tensor_forward_multiply(1, group)
                 keep_summed_chunks(1, group)
-            forward_level_2(1)
+            forward_level_2(1, [DIFFERENCE])
             for s in range(UNITS + 3):
                 if (s + 13) % E_BLOCKS == 0 and is_tile((s + 13) // E_BLOCKS):
                     load((s + 13) // E_BLOCKS)
@@ -506,7 +523,7 @@ def tile_waveletgatednet_kernel(tc, x, W_words, W_scales, b, threshold, out):
                 if is_unit(s - 3):
                     add_residual_and_store(s - 3)
                 if is_unit(s - 1):
-                    difference_n1(s - 1)
+                    difference_n1(nc.vector if s < 3 else nc.gpsimd, s - 1)
                 if is_unit(s - 1) and both_levels_on_tensor(s - 1):
                     sum_n1(nc.gpsimd, s - 1, slice(2, 4))
                 if is_unit(s - 1) and not both_levels_on_tensor(s - 1):
@@ -516,7 +533,6 @@ def tile_waveletgatednet_kernel(tc, x, W_words, W_scales, b, threshold, out):
                 for i, level in forward_jobs(s):
                     level(i)
                 if s == 0:
-                    round_rows(1, 1, on_vector=True)
                     round_rows(1, 3, on_vector=True)
                 if is_unit(s + 1):
                     multiply(s + 1)

@@ -28,12 +28,18 @@ CHUNK_D = P // NODES
 BANK_CHUNKS = 4
 
 
-def tensor_groups(i):
-    return 4 if i == 0 else 3
+def tensor_chunks(i):
+    return 18 if i == 0 else 12
+
+
+def chunk_groups(i):
+    return [
+        range(first, min(first + BANK_CHUNKS, tensor_chunks(i))) for first in range(0, tensor_chunks(i), BANK_CHUNKS)
+    ]
 
 
 def tensor_d(i):
-    return tensor_groups(i) * BANK_CHUNKS * CHUNK_D
+    return tensor_chunks(i) * CHUNK_D
 
 
 def tensor_l(i):
@@ -162,18 +168,17 @@ def tile_waveletgatednet_kernel(tc, x, W_words, W_scales, b, threshold, out):
 
 
         def tensor_forward_transpose(i, group):
-            first = group * BANK_CHUNKS
-            flipped = psum.tile([P, BANK_CHUNKS, P], BF16, tag="flipped")
-            for c in range(BANK_CHUNKS):
+            chunks = chunk_groups(i)[group]
+            flipped = psum.tile([P, len(chunks), P], BF16, tag="flipped")
+            for place, chunk in enumerate(chunks):
                 nc.tensor.transpose(
-                    flipped[:, c, :],
-                    x_tiles[i][:, (first + c) * P : (first + c + 1) * P],
-                    ident_bf16[:],
+                    flipped[:, place, :], x_tiles[i][:, chunk * P : (chunk + 1) * P], ident_bf16[:]
                 )
             flipped_chunks[i, group] = flipped
 
         def keep_flipped_chunks(i, group):
-            x_t[i, group] = sbuf.tile([P, BANK_CHUNKS, P], BF16, tag="x_t", bufs=2, name="x_t_tile")
+            chunks = chunk_groups(i)[group]
+            x_t[i, group] = sbuf.tile([P, len(chunks), P], BF16, tag="x_t", bufs=2, name="x_t_tile")
             nc.scalar.copy(out=x_t[i, group][:], in_=flipped_chunks[i, group][:])
 
         def new_coeffs(i):
@@ -182,12 +187,12 @@ def tile_waveletgatednet_kernel(tc, x, W_words, W_scales, b, threshold, out):
 
         def tensor_forward_multiply(i, group):
             new_coeffs(i)
-            first = group * BANK_CHUNKS
-            summed = psum.tile([P, BANK_CHUNKS, NODES, CHUNK_D], F32, tag="z_t")
-            for c in range(BANK_CHUNKS):
+            chunks = chunk_groups(i)[group]
+            summed = psum.tile([P, len(chunks), NODES, CHUNK_D], F32, tag="z_t")
+            for place in range(len(chunks)):
                 nc.tensor.matmul(
-                    out=summed[:, c, :, :].rearrange("p n d -> p (n d)"),
-                    lhsT=x_t[i, group][:, c, :],
+                    out=summed[:, place, :, :].rearrange("p n d -> p (n d)"),
+                    lhsT=x_t[i, group][:, place, :],
                     rhs=haar[:].rearrange("p g b d -> p (g b d)"),
                     start=True,
                     stop=True,
@@ -195,10 +200,10 @@ def tile_waveletgatednet_kernel(tc, x, W_words, W_scales, b, threshold, out):
             summed_chunks[i, group] = summed
 
         def keep_summed_chunks(i, group):
-            first = group * BANK_CHUNKS
-            d_range = slice(first * CHUNK_D, (first + BANK_CHUNKS) * CHUNK_D)
+            chunks = chunk_groups(i)[group]
+            d_range = slice(chunks[0] * CHUNK_D, (chunks[-1] + 1) * CHUNK_D)
             nc.scalar.copy(
-                out=coeffs[i][:, :, d_range].rearrange("p n (c d) -> p n c d", c=BANK_CHUNKS),
+                out=coeffs[i][:, :, d_range].rearrange("p n (c d) -> p n c d", c=len(chunks)),
                 in_=summed_chunks[i, group][:].rearrange("p c n d -> p n c d"),
             )
 
@@ -354,12 +359,19 @@ def tile_waveletgatednet_kernel(tc, x, W_words, W_scales, b, threshold, out):
             )
 
 
+        def made_before(u, j0):
+            return not both_levels_on_tensor(u) and (j0 == 1 or u == UNITS - 1)
+
         def half_n1(u, j0):
             first = 4 * (1 - j0)
             return after_n1[u][:, first : first + NODES // 2, :]
 
+        def half_n2(u, j0):
+            first = NODES + 4 * (1 - j0)
+            return after_n1[u][:, first : first + NODES // 2, :]
+
         def difference_n1(engine, u):
-            planes = NODES if both_levels_on_tensor(u) else NODES + 4
+            planes = NODES + 4 * (made_before(u, 1) + made_before(u, 0))
             after_n1[u] = sbuf.tile([P, planes, P], F32, tag="after_n1", bufs=3, name="after_n1_tile")
             engine.tensor_tensor(
                 out=half_n1(u, 1), in0=kept[u][:, 0:4, :], in1=kept[u][:, 4:8, :], op=ALU.subtract
@@ -369,11 +381,11 @@ def tile_waveletgatednet_kernel(tc, x, W_words, W_scales, b, threshold, out):
             low, high = (kept[u][:, first : first + NODES // 2, :][:, planes, :] for first in (0, NODES // 2))
             engine.tensor_tensor(out=half_n1(u, 0)[:, planes, :], in0=low, in1=high, op=ALU.add)
 
-        def level_n2_of_half(engine, u, j1):
+        def level_n2(engine, u, j0, j1):
             engine.tensor_tensor(
-                out=after_n1[u][:, NODES + 2 * j1 : NODES + 2 * j1 + 2, :],
-                in0=half_n1(u, 1)[:, 0:2, :],
-                in1=half_n1(u, 1)[:, 2:4, :],
+                out=half_n2(u, j0)[:, 2 * j1 : 2 * j1 + 2, :],
+                in0=half_n1(u, j0)[:, 0:2, :],
+                in1=half_n1(u, j0)[:, 2:4, :],
                 op=ALU.add if j1 == 0 else ALU.subtract,
             )
 
@@ -381,31 +393,27 @@ def tile_waveletgatednet_kernel(tc, x, W_words, W_scales, b, threshold, out):
         def negate(u, j0):
             if j0 == 1:
                 negated[u] = sbuf.tile([P, 2, 3, P], F32, tag="negated", bufs=2, name="negated_tile")
-            if j0 == 0 or both_levels_on_tensor(u):
-                nc.scalar.mul(out=negated[u][:, j0, :, :], in_=half_n1(u, j0)[:, 1:4, :], mul=-1.0)
+            if made_before(u, j0):
+                odd = half_n2(u, j0).rearrange("p (j c) r -> p j c r", c=2)[:, :, 1, :]
+                nc.scalar.mul(out=negated[u][:, j0, 0:2, :], in_=odd, mul=-1.0)
             else:
-                nc.scalar.mul(
-                    out=negated[u][:, j0, 0:2, :],
-                    in_=after_n1[u][:, NODES : NODES + 4, :].rearrange("p (j c) r -> p j c r", c=2)[:, :, 1, :],
-                    mul=-1.0,
-                )
+                nc.scalar.mul(out=negated[u][:, j0, :, :], in_=half_n1(u, j0)[:, 1:4, :], mul=-1.0)
 
         def terms_of_plane(u, j2, j1, j0):
-            if j0 == 0 or both_levels_on_tensor(u):
+            if made_before(u, j0):
                 return [
-                    negated[u][:, j0, term - 1, :]
-                    if ((term // 2) * j1 + (term % 2) * j2) % 2 == 1
-                    else half_n1(u, j0)[:, term, :]
-                    for term in range(4)
+                    half_n2(u, j0)[:, 2 * j1, :],
+                    negated[u][:, j0, j1, :] if j2 == 1 else half_n2(u, j0)[:, 2 * j1 + 1, :],
                 ]
-            first = NODES + 2 * j1
             return [
-                after_n1[u][:, first, :],
-                negated[u][:, j0, j1, :] if j2 == 1 else after_n1[u][:, first + 1, :],
+                negated[u][:, j0, term - 1, :]
+                if ((term // 2) * j1 + (term % 2) * j2) % 2 == 1
+                else half_n1(u, j0)[:, term, :]
+                for term in range(4)
             ]
 
         def inverse_levels_n2_n3(u, j2):
-            bank = psum.tile([P, 4, P], F32, tag="back", name="back_bank")
+            bank = psum.tile([P, 4, P], F32, tag="coeffs_t" if u == UNITS - 2 else "back", name="back_bank")
             for j0 in (1, 0):
                 for j1 in range(2):
                     terms = terms_of_plane(u, j2, j1, j0)
@@ -425,17 +433,24 @@ def tile_waveletgatednet_kernel(tc, x, W_words, W_scales, b, threshold, out):
             unit_samples = slice(k * P * NODES, (k + 1) * P * NODES)
             samples = x_tiles[i][:, unit_samples].rearrange("p (d h j) -> p d h j", h=2, j=4)
             result = sbuf.tile([P, P, 2, 4], F32, tag="result", bufs=3)
-            for j2 in range(2):
+
+            def add_residual(j2, d):
                 nc.vector.tensor_tensor(
-                    out=result[:, :, j2, :],
-                    in0=back[u, j2][:].rearrange("p j d -> p d j"),
-                    in1=samples[:, :, j2, :],
+                    out=result[:, d, j2, :],
+                    in0=back[u, j2][:].rearrange("p j d -> p d j")[:, d, :],
+                    in1=samples[:, d, j2, :],
                     op=ALU.add,
                 )
-            nc.sync.dma_start(
-                out=out_rows[i * P : (i + 1) * P, unit_samples],
-                in_=result[:].rearrange("p d h j -> p (d h j)"),
-            )
+
+            add_residual(0, slice(0, P))
+            width = P // 2 if u == UNITS - 1 else P
+            for first in range(0, P, width):
+                d = slice(first, first + width)
+                add_residual(1, d)
+                nc.sync.dma_start(
+                    out=out_rows[i * P : (i + 1) * P, unit_samples][:, first * NODES : (first + width) * NODES],
+                    in_=result[:, d, :, :].rearrange("p d h j -> p (d h j)"),
+                )
 
         def both_levels_on_tensor(u):
             return u + 1 <= LAST_FORWARD_STEP
@@ -451,7 +466,7 @@ def tile_waveletgatednet_kernel(tc, x, W_words, W_scales, b, threshold, out):
             if s in (0, 1, 2):
                 return [(2, s)]
             i, group = divmod(s + 9, E_BLOCKS)
-            return [(i, group)] if is_tile(i) and group < tensor_groups(i) else []
+            return [(i, group)] if is_tile(i) and group < len(chunk_groups(i)) else []
 
         def pairs_to_round(s):
             early = {0: [(1, 0), (1, 1), (1, 2)], 1: [], 2: [(2, 0)], 3: [(2, 1), (2, 2)], 4: [(2, 3)]}
@@ -478,7 +493,7 @@ def tile_waveletgatednet_kernel(tc, x, W_words, W_scales, b, threshold, out):
             load(3)
             for level in (forward_level_1, forward_level_2, forward_level_3):
                 level(0)
-            groups = [(0, group) for group in range(tensor_groups(0))] + [(1, 0)]
+            groups = [(0, group) for group in range(len(chunk_groups(0)))] + [(1, 0)]
             for number, group in enumerate(groups):
                 tensor_forward_transpose(*group)
                 keep_flipped_chunks(*group)
@@ -522,12 +537,13 @@ def tile_waveletgatednet_kernel(tc, x, W_words, W_scales, b, threshold, out):
                     square(s)
                 if is_unit(s - 3):
                     add_residual_and_store(s - 3)
-                if is_unit(s - 1):
+                if s == UNITS:
+                    for j0 in (1, 0):
+                        for j1 in range(2):
+                            level_n2(nc.vector, s - 1, j0, j1)
+                if is_unit(s - 1) and s < UNITS:
                     difference_n1(nc.vector if s < 3 else nc.gpsimd, s - 1)
-                if is_unit(s - 1) and both_levels_on_tensor(s - 1):
                     sum_n1(nc.gpsimd, s - 1, slice(2, 4))
-                if is_unit(s - 1) and not both_levels_on_tensor(s - 1):
-                    level_n2_of_half(nc.gpsimd, s - 1, 1)
                 if (s + 2) % E_BLOCKS == 0 and is_tile((s + 2) // E_BLOCKS):
                     quantise((s + 2) // E_BLOCKS)
                 for i, level in forward_jobs(s):
@@ -542,10 +558,10 @@ def tile_waveletgatednet_kernel(tc, x, W_words, W_scales, b, threshold, out):
                     keep_flipped_chunks(*tile_and_group)
                 if is_unit(s - 2):
                     negate(s - 2, 0)
-                if is_unit(s + 1):
-                    transpose_coeffs(s + 1)
                 for tile_and_pair in pairs_to_transpose(s)[:1]:
                     transpose_rounded(*tile_and_pair)
+                if is_unit(s + 1):
+                    transpose_coeffs(s + 1)
                 for tile_and_group in groups_to_transform(s):
                     tensor_forward_multiply(*tile_and_group)
                 if is_unit(s + 1):
@@ -562,10 +578,13 @@ def tile_waveletgatednet_kernel(tc, x, W_words, W_scales, b, threshold, out):
                     keep_flipped_pair(*tile_and_pair)
                 if is_unit(s - 2):
                     inverse_levels_n2_n3(s - 2, 1)
-                if is_unit(s - 1) and both_levels_on_tensor(s - 1):
+                if is_unit(s - 1) and s < UNITS:
                     sum_n1(nc.vector, s - 1, slice(0, 2))
-                if is_unit(s - 1) and not both_levels_on_tensor(s - 1):
-                    sum_n1(nc.vector, s - 1)
-                    level_n2_of_half(nc.vector, s - 1, 0)
+                if is_unit(s - 1) and s < UNITS and not both_levels_on_tensor(s - 1):
+                    level_n2(nc.vector, s - 1, 1, 0)
+                    level_n2(nc.vector, s - 1, 1, 1)
                 if is_unit(s):
                     keep_large(s)
+                if s == UNITS - 1:
+                    difference_n1(nc.vector, s)
+                    sum_n1(nc.vector, s)

@@ -234,27 +234,22 @@ def tile_waveletgatednet_kernel(tc, x, W_words, W_scales, b, threshold, out):
 
         def round_rows(i, pair, on_vector=False):
             if i not in rounded:
-                rounded[i] = sbuf.tile([P, NODES, D], BF16, tag="rounded", bufs=2, name="rounded_tile")
-            nodes = slice(2 * pair, 2 * pair + 2)
+                rounded[i] = sbuf.tile([P, PAIRS, 2, 2 * P, 2], BF16, tag="rounded", bufs=2, name="rounded_tile")
+            out = rounded[i][:, pair, :, :, :]
+            in_ = coeffs[i][:, 2 * pair : 2 * pair + 2, :].rearrange("p n (q h e) -> p h (n q) e", h=2, e=2)
             if on_vector:
-                nc.vector.tensor_scalar(
-                    out=rounded[i][:, nodes, :],
-                    in0=coeffs[i][:, nodes, :],
-                    scalar1=8.0 ** -0.5,
-                    scalar2=None,
-                    op0=ALU.mult,
-                )
+                nc.vector.tensor_scalar(out=out, in0=in_, scalar1=8.0 ** -0.5, scalar2=None, op0=ALU.mult)
             else:
-                nc.scalar.activation(
-                    out=rounded[i][:, nodes, :], in_=coeffs[i][:, nodes, :], func=ACT.Copy, scale=8.0 ** -0.5
-                )
+                nc.scalar.activation(out=out, in_=in_, func=ACT.Copy, scale=8.0 ** -0.5)
 
         def transpose_rounded(i, pair):
             flipped = psum.tile([P, 2, 2, P], F32, tag="flipped")
             for n in range(2):
-                as_words = rounded[i][:, 2 * pair + n, :].bitcast(F32)
                 for h in range(2):
-                    nc.tensor.transpose(flipped[:, n, h, :], as_words[:, h : D // 2 : 2], ident_f32[:])
+                    values = rounded[i][:, pair, h, n * P : (n + 1) * P, :]
+                    nc.tensor.transpose(
+                        flipped[:, n, h, :], values.rearrange("p q e -> p (q e)").bitcast(F32), ident_f32[:]
+                    )
             flipped_pairs[i, pair] = flipped
 
         def keep_flipped_pair(i, pair):
@@ -578,13 +573,13 @@ def tile_waveletgatednet_kernel(tc, x, W_words, W_scales, b, threshold, out):
                     keep_flipped_pair(*tile_and_pair)
                 if is_unit(s - 2):
                     inverse_levels_n2_n3(s - 2, 1)
-                if is_unit(s - 1) and s < UNITS:
-                    sum_n1(nc.vector, s - 1, slice(0, 2))
                 if is_unit(s - 1) and s < UNITS and not both_levels_on_tensor(s - 1):
                     level_n2(nc.vector, s - 1, 1, 0)
                     level_n2(nc.vector, s - 1, 1, 1)
                 if is_unit(s):
                     keep_large(s)
+                if is_unit(s - 1) and s < UNITS:
+                    sum_n1(nc.vector, s - 1, slice(0, 2))
                 if s == UNITS - 1:
                     difference_n1(nc.vector, s)
                     sum_n1(nc.vector, s)

@@ -235,8 +235,8 @@ def tile_waveletgatednet_kernel(tc, x, W_words, W_scales, b, threshold, out):
         def round_rows(i, pair, on_vector=False):
             if i not in rounded:
                 rounded[i] = sbuf.tile([P, PAIRS, 2, 2 * P, 2], BF16, tag="rounded", bufs=2, name="rounded_tile")
-            out = rounded[i][:, pair, :, :, :]
-            in_ = coeffs[i][:, 2 * pair : 2 * pair + 2, :].rearrange("p n (q h e) -> p h (n q) e", h=2, e=2)
+            out = rounded[i][:, pair, :, :, :].rearrange("p h m e -> p m h e")
+            in_ = coeffs[i][:, 2 * pair : 2 * pair + 2, :].rearrange("p n (q h e) -> p (n q) h e", h=2, e=2)
             if on_vector:
                 nc.vector.tensor_scalar(out=out, in0=in_, scalar1=8.0 ** -0.5, scalar2=None, op0=ALU.mult)
             else:

@@ -56,15 +56,16 @@ FLOPS = 2 * ROWS * NODES * D * D
 SUM, DIFFERENCE = 0, 1
 
 
-def forward_level(nc, out, in_, halves=(SUM, DIFFERENCE)):
-    pairs = in_.rearrange("p g (m two) -> p g two m", two=2)
+def butterfly(nc, outs, first, second, halves=(SUM, DIFFERENCE)):
     for half in halves:
         nc.vector.tensor_tensor(
-            out=out[:, :, half, :],
-            in0=pairs[:, :, 0, :],
-            in1=pairs[:, :, 1, :],
-            op=ALU.add if half == SUM else ALU.subtract,
+            out=outs[half], in0=first, in1=second, op=ALU.add if half == SUM else ALU.subtract
         )
+
+
+def forward_level(nc, out, in_):
+    pairs = in_.rearrange("p g (m two) -> p g two m", two=2)
+    butterfly(nc, (out[:, :, SUM, :], out[:, :, DIFFERENCE, :]), pairs[:, :, 0, :], pairs[:, :, 1, :])
 
 
 def tile_waveletgatednet_kernel(tc, x, W_words, W_scales, b, threshold, out):
@@ -207,22 +208,24 @@ def tile_waveletgatednet_kernel(tc, x, W_words, W_scales, b, threshold, out):
                 in_=summed_chunks[i, group][:].rearrange("p c n d -> p n c d"),
             )
 
+
         def forward_level_1(i):
             pieces = FIRST_PIECES if i == 0 else 1
-            outputs = (L - tensor_l(i)) // 2
-            level1[i] = sbuf.tile([P, 1, 2, outputs], F32, tag="level1", name="level1_tile")
+            outputs = (L - tensor_l(i)) // 4
+            level1[i] = sbuf.tile([P, 2, 2, outputs], F32, tag="level1", name="level1_tile")
             step = outputs // pieces
             for m in range(0, outputs, step):
-                first = tensor_l(i) + 2 * m
-                forward_level(
-                    nc, level1[i][:, :, :, m : m + step], x_tiles[i][:, first : first + 2 * step].unsqueeze(1)
-                )
+                first = tensor_l(i) + 4 * m
+                pairs = x_tiles[i][:, first : first + 4 * step].rearrange("p (m q two) -> p q two m", q=2, two=2)
+                outs = [level1[i][:, half, :, m : m + step] for half in (SUM, DIFFERENCE)]
+                butterfly(nc, outs, pairs[:, :, 0, :], pairs[:, :, 1, :])
 
         def forward_level_2(i, halves=(SUM, DIFFERENCE)):
             if i not in level2:
                 outputs = (L - tensor_l(i)) // 4
                 level2[i] = sbuf.tile([P, 2, 2, outputs], F32, tag="level2", name="level2_tile")
-            forward_level(nc, level2[i][:], level1[i][:].rearrange("p g b m -> p (g b) m"), halves)
+            outs = [level2[i][:, :, half, :] for half in (SUM, DIFFERENCE)]
+            butterfly(nc, outs, level1[i][:, :, 0, :], level1[i][:, :, 1, :], halves)
 
         def forward_level_3(i):
             new_coeffs(i)

@@ -467,7 +467,7 @@ def tile_waveletgatednet_kernel(tc, x, W_words, W_scales, b, threshold, out):
             return [(i, group)] if is_tile(i) and group < len(chunk_groups(i)) else []
 
         def pairs_to_round(s):
-            early = {0: [(1, 0), (1, 1), (1, 2)], 1: [], 2: [(2, 0)], 3: [(2, 1), (2, 2)], 4: [(2, 3)]}
+            early = {0: [(1, 0), (1, 1), (1, 2)], 1: [], 2: [(2, 0), (2, 1)], 3: [(2, 2)], 4: [(2, 3)]}
             if s in early:
                 return early[s]
             i, pair = divmod(s + 7, PAIRS)
@@ -566,14 +566,14 @@ def tile_waveletgatednet_kernel(tc, x, W_words, W_scales, b, threshold, out):
                     sigmoid(s + 1, 1)
                 for tile_and_group in groups_to_transform(s):
                     keep_summed_chunks(*tile_and_group)
-                for tile_and_pair in pairs_to_round(s):
-                    round_rows(*tile_and_pair)
                 if is_unit(s - 2):
                     inverse_levels_n2_n3(s - 2, 0)
                 for number, tile_and_pair in enumerate(pairs_to_transpose(s)):
                     if number > 0:
                         transpose_rounded(*tile_and_pair)
                     keep_flipped_pair(*tile_and_pair)
+                for tile_and_pair in pairs_to_round(s):
+                    round_rows(*tile_and_pair)
                 if is_unit(s - 2):
                     inverse_levels_n2_n3(s - 2, 1)
                 if is_unit(s - 1) and s < UNITS and not both_levels_on_tensor(s - 1):

from contextlib import ExitStack

import concourse.mybir as mybir
from concourse.masks import make_identity

F32 = mybir.dt.float32
BF16 = mybir.dt.bfloat16
I32 = mybir.dt.int32
U32 = mybir.dt.uint32
U8 = mybir.dt.uint8
FP8X4 = mybir.dt.float8_e4m3fn_x4
ALU = mybir.AluOpType
ACT = mybir.ActivationFunctionType

P = 128
L = 4096
NODES = 8
D = L // NODES
PACK = 4
E_BLOCKS = D // P
N_MOVING = 512
ROWS = 64 * 16
ROW_TILES = ROWS // P
UNITS = ROW_TILES * E_BLOCKS
PAIRS = NODES // 2

CHUNK_D = P // NODES
BANK_CHUNKS = 4


def tensor_chunks(i):
    return 18 if i == 0 else 12


def chunk_groups(i):
    return [
        range(first, min(first + BANK_CHUNKS, tensor_chunks(i))) for first in range(0, tensor_chunks(i), BANK_CHUNKS)
    ]


def tensor_d(i):
    return tensor_chunks(i) * CHUNK_D


def tensor_l(i):
    return tensor_d(i) * NODES


LAST_FORWARD_STEP = (ROW_TILES - 1) * E_BLOCKS - 7

FIRST_PIECES = 2

FLOPS = 2 * ROWS * NODES * D * D


SUM, DIFFERENCE = 0, 1


def butterfly(nc, outs, first, second, halves=(SUM, DIFFERENCE)):
    for half in halves:
        nc.vector.tensor_tensor(
            out=outs[half], in0=first, in1=second, op=ALU.add if half == SUM else ALU.subtract
        )


def forward_level(nc, out, in_):
    pairs = in_.rearrange("p g (m two) -> p g two m", two=2)
    butterfly(nc, (out[:, :, SUM, :], out[:, :, DIFFERENCE, :]), pairs[:, :, 0, :], pairs[:, :, 1, :])


def tile_waveletgatednet_kernel(tc, x, W_words, W_scales, b, threshold, out):
    nc = tc.nc
    x_rows = x.flatten_outer_dims()
    out_rows = out.flatten_outer_dims()

    with ExitStack() as ctx:
        const = ctx.enter_context(tc.tile_pool(name="const", bufs=1))
        sbuf = ctx.enter_context(tc.tile_pool(name="sbuf", bufs=1))
        psum = ctx.enter_context(tc.psum_pool(name="psum", bufs=2))

        x_tiles = {}

        def load(i):
            x_tiles[i] = sbuf.tile([P, L], BF16, tag="x", bufs=5, name="x_tile")
            pieces = FIRST_PIECES if i == 0 else 1
            samples = (L - tensor_l(i)) // pieces
            parts = [slice(first, first + samples) for first in range(tensor_l(i), L, samples)]
            for part in parts + [slice(0, tensor_l(i))]:
                nc.sync.dma_start(out=x_tiles[i][:, part], in_=x_rows[i * P : (i + 1) * P, part])

        load(0)
        load(1)

        ident_f32 = const.tile([P, P], F32)
        make_identity(nc, ident_f32[:])
        ident_bf16 = const.tile([P, P], BF16)
        make_identity(nc, ident_bf16[:])

        haar1 = const.tile([P, 1, 2, P // 2], F32)
        haar2 = const.tile([P, 2, 2, P // 4], F32)
        haar = const.tile([P, 4, 2, CHUNK_D], BF16)

        def make_haar():
            forward_level(nc, haar1[:], ident_f32[:].unsqueeze(1))
            forward_level(nc, haar2[:], haar1[:].rearrange("p g b m -> p (g b) m"))
            forward_level(nc, haar[:], haar2[:].rearrange("p g b m -> p (g b) m"))

        w_codes = const.tile([P, D], U32, align_bytes=64)
        nc.sync.dma_start(
            out=w_codes[:].bitcast(I32),
            in_=W_words[0].rearrange("p e t -> p (e t)").bitcast(I32),
        )
        w_scales = const.tile([P, D], U8, align_bytes=64)
        nc.vector.memset(w_scales[:].bitcast(I32), 0)
        for quadrant in range(4):
            nc.sync.dma_start(
                out=w_scales[32 * quadrant : 32 * quadrant + 4, :].bitcast(I32),
                in_=W_scales[0, 4 * quadrant : 4 * quadrant + 4, :].bitcast(I32),
            )

        b_rows = const.tile([P, P], BF16)
        nc.vector.memset(b_rows[:], 0.0)
        nc.sync.dma_start(out=b_rows[0:E_BLOCKS, :], in_=b.rearrange("(k e) -> k e", e=P))
        bias = const.tile([P, E_BLOCKS], F32)

        thr_bf16 = const.tile([P, 1], BF16)
        nc.sync.dma_start(out=thr_bf16[:], in_=threshold.partition_broadcast(P))
        thr = const.tile([P, 1], F32)
        thr_sq = const.tile([P, 1], F32)

        def transpose_bias():
            b_cols = psum.tile([P, P], BF16, tag="flipped")
            nc.tensor.transpose(b_cols[:], b_rows[:], ident_bf16[:])
            nc.scalar.copy(out=bias[:], in_=b_cols[:, 0:E_BLOCKS])

        def finish_threshold():
            nc.vector.tensor_copy(out=thr[:], in_=thr_bf16[:])
            nc.vector.scalar_tensor_tensor(
                out=thr_sq[:], in0=thr[:], scalar=0.125, in1=thr[:], op0=ALU.mult, op1=ALU.mult
            )

        def load_sigmoid_table():
            nc.vector.memset(thr_sq[:], 0.0)
            nc.scalar.activation(out=thr_sq[:], in_=thr_sq[:], func=ACT.Sigmoid)

        level1 = {}
        level2 = {}
        coeffs = {}
        rounded = {}
        grouped = {}
        x_t = {}
        words = {}
        scales = {}
        gates_t = {}
        coeffs_t = {}
        product = {}
        squared = {}
        kept = {}
        after_n1 = {}
        negated = {}
        flipped_chunks = {}
        summed_chunks = {}
        flipped_pairs = {}
        z_t = {}
        back = {}

        def unit_tile(tag, bufs):
            return sbuf.tile([P, NODES, P], F32, tag=tag, bufs=bufs, name=tag + "_tile")


        def tensor_forward_transpose(i, group):
            chunks = chunk_groups(i)[group]
            flipped = psum.tile([P, len(chunks), P], BF16, tag="flipped")
            for place, chunk in enumerate(chunks):
                nc.tensor.transpose(
                    flipped[:, place, :], x_tiles[i][:, chunk * P : (chunk + 1) * P], ident_bf16[:]
                )
            flipped_chunks[i, group] = flipped

        def keep_flipped_chunks(i, group):
            chunks = chunk_groups(i)[group]
            x_t[i, group] = sbuf.tile([P, len(chunks), P], BF16, tag="x_t", bufs=2, name="x_t_tile")
            nc.scalar.copy(out=x_t[i, group][:], in_=flipped_chunks[i, group][:])

        def new_coeffs(i):
            if i not in coeffs:
                coeffs[i] = sbuf.tile([P, NODES, D], F32, tag="coeffs", bufs=3, name="coeffs_tile")

        def tensor_forward_multiply(i, group):
            new_coeffs(i)
            chunks = chunk_groups(i)[group]
            summed = psum.tile([P, len(chunks), NODES, CHUNK_D], F32, tag="z_t")
            for place in range(len(chunks)):
                nc.tensor.matmul(
                    out=summed[:, place, :, :].rearrange("p n d -> p (n d)"),
                    lhsT=x_t[i, group][:, place, :],
                    rhs=haar[:].rearrange("p g b d -> p (g b d)"),
                    start=True,
                    stop=True,
                )
            summed_chunks[i, group] = summed

        def keep_summed_chunks(i, group):
            chunks = chunk_groups(i)[group]
            d_range = slice(chunks[0] * CHUNK_D, (chunks[-1] + 1) * CHUNK_D)
            nc.scalar.copy(
                out=coeffs[i][:, :, d_range].rearrange("p n (c d) -> p n c d", c=len(chunks)),
                in_=summed_chunks[i, group][:].rearrange("p c n d -> p n c d"),
            )


        def forward_level_1(i):
            pieces = FIRST_PIECES if i == 0 else 1
            outputs = (L - tensor_l(i)) // 4
            level1[i] = sbuf.tile([P, 2, 2, outputs], F32, tag="level1", name="level1_tile")
            step = outputs // pieces
            for m in range(0, outputs, step):
                first = tensor_l(i) + 4 * m
                pairs = x_tiles[i][:, first : first + 4 * step].rearrange("p (m q two) -> p q two m", q=2, two=2)
                outs = [level1[i][:, half, :, m : m + step] for half in (SUM, DIFFERENCE)]
                butterfly(nc, outs, pairs[:, :, 0, :], pairs[:, :, 1, :])

        def forward_level_2(i, halves=(SUM, DIFFERENCE)):
            if i not in level2:
                outputs = (L - tensor_l(i)) // 4
                level2[i] = sbuf.tile([P, 2, 2, outputs], F32, tag="level2", name="level2_tile")
            outs = [level2[i][:, :, half, :] for half in (SUM, DIFFERENCE)]
            butterfly(nc, outs, level1[i][:, :, 0, :], level1[i][:, :, 1, :], halves)

        def forward_level_3(i):
            new_coeffs(i)
            forward_level(
                nc,
                coeffs[i][:, :, tensor_d(i) : D].rearrange("p (g b) d -> p g b d", b=2),
                level2[i][:].rearrange("p g b m -> p (g b) m"),
            )

        def round_rows(i, pair, on_vector=False):
            if i not in rounded:
                rounded[i] = sbuf.tile([P, PAIRS, 2, 2 * P, 2], BF16, tag="rounded", bufs=2, name="rounded_tile")
            out = rounded[i][:, pair, :, :, :].rearrange("p h m e -> p m h e")
            in_ = coeffs[i][:, 2 * pair : 2 * pair + 2, :].rearrange("p n (q h e) -> p (n q) h e", h=2, e=2)
            if on_vector:
                nc.vector.tensor_scalar(out=out, in0=in_, scalar1=8.0 ** -0.5, scalar2=None, op0=ALU.mult)
            else:
                nc.scalar.activation(out=out, in_=in_, func=ACT.Copy, scale=8.0 ** -0.5)

        def transpose_rounded(i, pair):
            flipped = psum.tile([P, 2, 2, P], F32, tag="flipped")
            for n in range(2):
                for h in range(2):
                    values = rounded[i][:, pair, h, n * P : (n + 1) * P, :]
                    nc.tensor.transpose(
                        flipped[:, n, h, :], values.rearrange("p q e -> p (q e)").bitcast(F32), ident_f32[:]
                    )
            flipped_pairs[i, pair] = flipped

        def keep_flipped_pair(i, pair):
            if i not in grouped:
                grouped[i] = sbuf.tile(
                    [P, NODES, P, PACK], BF16, tag="grouped", bufs=2, align_bytes=64, name="grouped_tile"
                )
            grouped_words = (
                grouped[i][:]
                .rearrange("p n r t -> p (n r t)")
                .bitcast(F32)
                .rearrange("p (n r h) -> p n r h", n=NODES, h=2)
            )
            nc.scalar.copy(
                out=grouped_words[:, 2 * pair : 2 * pair + 2, :, :],
                in_=flipped_pairs[i, pair][:].rearrange("p n h r -> p n r h"),
            )

        def quantise(i):
            words[i] = sbuf.tile(
                [P, NODES * P], U32, tag="words", bufs=2, align_bytes=64, name="words_tile"
            )
            scales[i] = sbuf.tile(
                [P, NODES * P], U8, tag="scales", bufs=2, align_bytes=64, name="scales_tile"
            )
            nc.vector.quantize_mx(
                out=words[i][:].bitcast(FP8X4),
                scales=scales[i][:],
                in_=grouped[i][:].rearrange("p n r t -> p (n r t)"),
            )


        def multiply(u):
            i, k = divmod(u, E_BLOCKS)
            e_cols = slice(k * P, (k + 1) * P)
            z_t[u] = []
            for c in range(NODES * P // N_MOVING):
                cols = slice(c * N_MOVING, (c + 1) * N_MOVING)
                bank = psum.tile([P, N_MOVING], F32, tag="z_t", name="z_t_bank")
                nc.tensor.matmul_mx(
                    out=bank[:],
                    lhsT=w_codes[:, e_cols].bitcast(FP8X4),
                    lhsT_scale=w_scales[:, e_cols],
                    rhs=words[i][:, cols].bitcast(FP8X4),
                    rhs_scale=scales[i][:, cols],
                    start=True,
                    stop=True,
                )
                z_t[u].append(bank)

        def sigmoid(u, c):
            k = u % E_BLOCKS
            if c == 0:
                gates_t[u] = unit_tile("gates_t", 2)
            nc.scalar.activation(
                out=gates_t[u][:].rearrange("p n r -> p (n r)")[:, c * N_MOVING : (c + 1) * N_MOVING],
                in_=z_t[u][c][:],
                func=ACT.Sigmoid,
                bias=bias[:, k : k + 1],
                scale=1.0,
            )

        def transpose_coeffs(u):
            i, k = divmod(u, E_BLOCKS)
            coeffs_t[u] = []
            for half in range(2):
                bank = psum.tile([P, NODES // 2, P], F32, tag="coeffs_t", name="coeffs_t_bank")
                for n in range(NODES // 2):
                    nc.tensor.transpose(
                        bank[:, n, :],
                        coeffs[i][:, half * (NODES // 2) + n, k * P : (k + 1) * P],
                        ident_f32[:],
                    )
                coeffs_t[u].append(bank)

        def gate_coeffs(u):
            product[u] = unit_tile("product", 2)
            for half in range(2):
                nodes = slice(half * (NODES // 2), (half + 1) * (NODES // 2))
                nc.vector.scalar_tensor_tensor(
                    out=product[u][:, nodes, :],
                    in0=coeffs_t[u][half][:],
                    scalar=0.125,
                    in1=gates_t[u][:, nodes, :],
                    op0=ALU.mult,
                    op1=ALU.mult,
                )

        def square(u):
            squared[u] = unit_tile("squared", 2)
            nc.scalar.activation(out=squared[u][:], in_=product[u][:], func=ACT.Square)

        def keep_large(u):
            kept[u] = unit_tile("kept", 2)
            nc.vector.scalar_tensor_tensor(
                out=kept[u][:],
                in0=squared[u][:],
                scalar=thr_sq[:, 0:1],
                in1=product[u][:],
                op0=ALU.is_ge,
                op1=ALU.mult,
            )


        def made_before(u, j0):
            return not both_levels_on_tensor(u) and (j0 == 1 or u == UNITS - 1)

        def half_n1(u, j0):
            first = 4 * (1 - j0)
            return after_n1[u][:, first : first + NODES // 2, :]

        def half_n2(u, j0):
            first = NODES + 4 * (1 - j0)
            return after_n1[u][:, first : first + NODES // 2, :]

        def difference_n1(engine, u):
            planes = NODES + 4 * (made_before(u, 1) + made_before(u, 0))
            after_n1[u] = sbuf.tile([P, planes, P], F32, tag="after_n1", bufs=3, name="after_n1_tile")
            engine.tensor_tensor(
                out=half_n1(u, 1), in0=kept[u][:, 0:4, :], in1=kept[u][:, 4:8, :], op=ALU.subtract
            )

        def sum_n1(engine, u, planes=slice(0, NODES // 2)):
            low, high = (kept[u][:, first : first + NODES // 2, :][:, planes, :] for first in (0, NODES // 2))
            engine.tensor_tensor(out=half_n1(u, 0)[:, planes, :], in0=low, in1=high, op=ALU.add)

        def level_n2(engine, u, j0, j1):
            engine.tensor_tensor(
                out=half_n2(u, j0)[:, 2 * j1 : 2 * j1 + 2, :],
                in0=half_n1(u, j0)[:, 0:2, :],
                in1=half_n1(u, j0)[:, 2:4, :],
                op=ALU.add if j1 == 0 else ALU.subtract,
            )


        def negate(u, j0):
            if j0 == 1:
                negated[u] = sbuf.tile([P, 2, 3, P], F32, tag="negated", bufs=2, name="negated_tile")
            if made_before(u, j0):
                odd = half_n2(u, j0).rearrange("p (j c) r -> p j c r", c=2)[:, :, 1, :]
                nc.scalar.mul(out=negated[u][:, j0, 0:2, :], in_=odd, mul=-1.0)
            else:
                nc.scalar.mul(out=negated[u][:, j0, :, :], in_=half_n1(u, j0)[:, 1:4, :], mul=-1.0)

        def terms_of_plane(u, j2, j1, j0):
            if made_before(u, j0):
                return [
                    half_n2(u, j0)[:, 2 * j1, :],
                    negated[u][:, j0, j1, :] if j2 == 1 else half_n2(u, j0)[:, 2 * j1 + 1, :],
                ]
            return [
                negated[u][:, j0, term - 1, :]
                if ((term // 2) * j1 + (term % 2) * j2) % 2 == 1
                else half_n1(u, j0)[:, term, :]
                for term in range(4)
            ]

        def inverse_levels_n2_n3(u, j2):
            bank = psum.tile([P, 4, P], F32, tag="coeffs_t" if u == UNITS - 2 else "back", name="back_bank")
            for j0 in (1, 0):
                for j1 in range(2):
                    terms = terms_of_plane(u, j2, j1, j0)
                    for number, term in enumerate(terms):
                        nc.tensor.matmul(
                            out=bank[:, 2 * j1 + j0, :],
                            lhsT=term,
                            rhs=ident_f32[:],
                            is_transpose=True,
                            start=(number == 0),
                            stop=(number == len(terms) - 1),
                        )
            back[u, j2] = bank

        def add_residual_and_store(u):
            i, k = divmod(u, E_BLOCKS)
            unit_samples = slice(k * P * NODES, (k + 1) * P * NODES)
            samples = x_tiles[i][:, unit_samples].rearrange("p (d h j) -> p d h j", h=2, j=4)
            result = sbuf.tile([P, P, 2, 4], F32, tag="result", bufs=3)

            def add_residual(j2, d):
                nc.vector.tensor_tensor(
                    out=result[:, d, j2, :],
                    in0=back[u, j2][:].rearrange("p j d -> p d j")[:, d, :],
                    in1=samples[:, d, j2, :],
                    op=ALU.add,
                )

            add_residual(0, slice(0, P))
            width = P // 2 if u == UNITS - 1 else P
            for first in range(0, P, width):
                d = slice(first, first + width)
                add_residual(1, d)
                nc.sync.dma_start(
                    out=out_rows[i * P : (i + 1) * P, unit_samples][:, first * NODES : (first + width) * NODES],
                    in_=result[:, d, :, :].rearrange("p d h j -> p (d h j)"),
                )

        def both_levels_on_tensor(u):
            return u + 1 <= LAST_FORWARD_STEP

        def forward_jobs(s):
            early = {0: [(1, forward_level_3)], 1: [(2, forward_level_1), (2, forward_level_2)], 2: [(2, forward_level_3)]}
            if s in early:
                return early[s]
            i, job = divmod(s + 9, E_BLOCKS)
            return [(i, (forward_level_1, forward_level_2, forward_level_3)[job])] if is_tile(i) and job < 3 else []

        def groups_to_transform(s):
            if s in (0, 1, 2):
                return [(2, s)]
            i, group = divmod(s + 9, E_BLOCKS)
            return [(i, group)] if is_tile(i) and group < len(chunk_groups(i)) else []

        def pairs_to_round(s):
            early = {0: [(1, 0), (1, 1), (1, 2)], 1: [], 2: [(2, 0), (2, 1)], 3: [(2, 2)], 4: [(2, 3)]}
            if s in early:
                return early[s]
            i, pair = divmod(s + 7, PAIRS)
            return [(i, pair)] if is_tile(i) else []

        def pairs_to_transpose(s):
            if s == 1:
                return [(1, 0), (1, 1), (1, 3), (1, 2)]
            return pairs_to_round(s - 1) if s > 0 else []

        def is_tile(i):
            return 0 <= i < ROW_TILES

        def is_unit(u):
            return 0 <= u < UNITS

        with tc.manual_schedule():
            make_haar()
            load_sigmoid_table()
            load(2)
            load(3)
            for level in (forward_level_1, forward_level_2, forward_level_3):
                level(0)
            groups = [(0, group) for group in range(len(chunk_groups(0)))] + [(1, 0)]
            for number, group in enumerate(groups):
                tensor_forward_transpose(*group)
                keep_flipped_chunks(*group)
                if number > 0:
                    tensor_forward_multiply(*groups[number - 1])
                    keep_summed_chunks(*groups[number - 1])
            tensor_forward_multiply(1, 0)
            transpose_coeffs(0)
            round_rows(0, 1, on_vector=True)
            round_rows(0, 3, on_vector=True)
            round_rows(0, 0)
            transpose_rounded(0, 1)
            keep_flipped_pair(0, 1)
            round_rows(0, 2)
            for pair in (3, 0, 2):
                transpose_rounded(0, pair)
                keep_flipped_pair(0, pair)
            keep_summed_chunks(1, 0)
            forward_level_1(1)
            finish_threshold()
            forward_level_2(1, [SUM])
            quantise(0)
            for group in (1, 2):
                tensor_forward_transpose(1, group)
                keep_flipped_chunks(1, group)
            transpose_bias()
            multiply(0)
            sigmoid(0, 0)
            sigmoid(0, 1)
            for group in (1, 2):
                tensor_forward_multiply(1, group)
                keep_summed_chunks(1, group)
            forward_level_2(1, [DIFFERENCE])
            for s in range(UNITS + 3):
                if (s + 13) % E_BLOCKS == 0 and is_tile((s + 13) // E_BLOCKS):
                    load((s + 13) // E_BLOCKS)
                if is_unit(s - 2):
                    negate(s - 2, 1)
                if is_unit(s):
                    gate_coeffs(s)
                    square(s)
                if is_unit(s - 3):
                    add_residual_and_store(s - 3)
                if s == UNITS:
                    for j0 in (1, 0):
                        for j1 in range(2):
                            level_n2(nc.vector, s - 1, j0, j1)
                if is_unit(s - 1) and s < UNITS:
                    difference_n1(nc.vector if s < 3 else nc.gpsimd, s - 1)
                    sum_n1(nc.gpsimd, s - 1, slice(2, 4))
                if (s + 2) % E_BLOCKS == 0 and is_tile((s + 2) // E_BLOCKS):
                    quantise((s + 2) // E_BLOCKS)
                for i, level in forward_jobs(s):
                    level(i)
                if s == 0:
                    round_rows(1, 3, on_vector=True)
                if is_unit(s + 1):
                    multiply(s + 1)
                    sigmoid(s + 1, 0)
                for tile_and_group in groups_to_transform(s):
                    tensor_forward_transpose(*tile_and_group)
                    keep_flipped_chunks(*tile_and_group)
                if is_unit(s - 2):
                    negate(s - 2, 0)
                for tile_and_pair in pairs_to_transpose(s)[:1]:
                    transpose_rounded(*tile_and_pair)
                if is_unit(s + 1):
                    transpose_coeffs(s + 1)
                for tile_and_group in groups_to_transform(s):
                    tensor_forward_multiply(*tile_and_group)
                if is_unit(s + 1):
                    sigmoid(s + 1, 1)
                for tile_and_group in groups_to_transform(s):
                    keep_summed_chunks(*tile_and_group)
                if is_unit(s - 2):
                    inverse_levels_n2_n3(s - 2, 0)
                for number, tile_and_pair in enumerate(pairs_to_transpose(s)):
                    if number > 0:
                        transpose_rounded(*tile_and_pair)
                    keep_flipped_pair(*tile_and_pair)
                for tile_and_pair in pairs_to_round(s):
                    round_rows(*tile_and_pair)
                if is_unit(s - 2):
                    inverse_levels_n2_n3(s - 2, 1)
                if is_unit(s - 1) and s < UNITS and not both_levels_on_tensor(s - 1):
                    level_n2(nc.vector, s - 1, 1, 0)
                    level_n2(nc.vector, s - 1, 1, 1)
                if is_unit(s):
                    keep_large(s)
                if is_unit(s - 1) and s < UNITS:
                    sum_n1(nc.vector, s - 1, slice(0, 2))
                if s == UNITS - 1:
                    difference_n1(nc.vector, s)
                    sum_n1(nc.vector, s)
